import numpy as np
import ml_dtypes


def mxq(x, axis, fmt="e4m3"):
    dtype, down = {"e4m3": (ml_dtypes.float8_e4m3fn, 7), "e5m2": (ml_dtypes.float8_e5m2, 14)}[fmt]
    v = np.moveaxis(np.asarray(x, np.float32).astype(ml_dtypes.bfloat16).astype(np.float64), axis, -1)
    blocks = v.reshape(v.shape[:-1] + (-1, 32))
    amax = np.abs(blocks).max(-1, keepdims=True)
    byte = np.maximum(np.where(amax > 0, np.frexp(amax)[1] - 1 + 127, 0) - down, 1)
    scale = np.exp2(byte - 127.0)
    codes = (blocks / scale).astype(np.float32).astype(dtype).astype(np.float64)
    return np.moveaxis((codes * scale).reshape(v.shape), -1, axis)


WIDE = False


def mx_kscale(k):
    if not WIDE:
        return np.ones(k)
    levels = np.array([10, -10, 5, -5, 0])
    a = np.random.permutation(np.resize(levels, k // 512 * 4)).reshape(k // 512, 4)
    idx = np.arange(k)
    return np.exp2(a[idx // 512, idx % 128 // 32])


BF16 = ml_dtypes.bfloat16


def bf(x):
    return np.asarray(x, np.float32).astype(BF16)


def f64(x):
    return np.asarray(x).astype(np.float64)


T, D = 1024, 1024


def setup_inputs():
    u = mx_kscale(T)
    b0 = np.random.standard_normal(D) * 0.5
    return {"err": bf((np.random.standard_normal((T, D)) * 1.7 + b0) * u[:, None]),
            "train_view": bf(np.random.standard_normal((T, D)) / u[:, None]),
            "test_view": bf(np.random.standard_normal((T, D))),
            "W": bf(np.random.standard_normal((D, D)) / np.sqrt(D)),
            "b": bf(b0),
            "lr_w": bf(np.random.uniform(size=(D, D)) * 0.25 * np.sqrt(T * D)),
            "lr_b": bf(np.random.uniform(size=D) * 0.5 * D / u.max())}


def reference(err, train_view, test_view, W, b, lr_w, lr_b):
    e = f64(err)
    coef = 2.0 / e.size
    gW = coef * (mxq(e, 0, "e4m3").T @ mxq(f64(train_view), 0, "e4m3"))
    gb = coef * e.sum(axis=0)
    W_new = f64(W) - f64(lr_w) * gW
    b_new = f64(b) - f64(lr_b) * gb
    q = f64(test_view)
    return (mxq(q, 1, "e4m3") @ mxq(W_new, 1, "e4m3").T) + b_new + q

@@ -1,0 +1,202 @@
+from contextlib import ExitStack
+
+import concourse.mybir as mybir
+from concourse.masks import make_identity
+
+F32 = mybir.dt.float32
+BF16 = mybir.dt.bfloat16
+U32 = mybir.dt.uint32
+U8 = mybir.dt.uint8
+FP8X4 = mybir.dt.float8_e4m3fn_x4
+ALU = mybir.AluOpType
+
+P = 128
+T = 1024
+D = 1024
+H = 512
+C = 2.0 / (T * D)
+FLOPS = 4 * T * D * D
+
+
+def tile_tttinner_pb_kernel(tc, err, train_view, test_view, W, b, lr_w, lr_b, out):
+    nc = tc.nc
+    with ExitStack() as ctx:
+        const = ctx.enter_context(tc.tile_pool(name="const", bufs=1))
+        rawp = ctx.enter_context(tc.tile_pool(name="rawp", bufs=6))
+        grp = ctx.enter_context(tc.tile_pool(name="grp", bufs=6))
+        gqp = ctx.enter_context(tc.tile_pool(name="gqp", bufs=2))
+        tmpp = ctx.enter_context(tc.tile_pool(name="tmpp", bufs=2))
+        ps = ctx.enter_context(tc.psum_pool(name="ps", bufs=4))
+
+        zr = const.tile([P, 2 * D], BF16)
+        nc.vector.memset(zr[:], 0.0)
+        ones = const.tile([P, P], BF16)
+        nc.vector.memset(ones[:], 1.0)
+        ident = const.tile([P, P], F32)
+        make_identity(nc, ident[:])
+        nc.scalar.dma_start(out=zr[0:1, 0:D], in_=b.rearrange("(o d) -> o d", o=1))
+        nc.scalar.dma_start(out=zr[0:1, D:2 * D], in_=lr_b.rearrange("(o d) -> o d", o=1))
+
+        def load(view, nm):
+            t = rawp.tile([P, 4, D], BF16, tag="raw", name=nm)
+            nc.sync.dma_start(out=t[:], in_=view)
+            return t
+
+        err_raw = []
+        trn_raw = []
+        for gt in range(2):
+            rows = slice(H * gt, H * gt + H)
+            err_raw.append(load(err[rows, :].rearrange("(p j) w -> p j w", j=4), "err_raw%d" % gt))
+            trn_raw.append(load(train_view[rows, :].rearrange("(p j) w -> p j w", j=4), "trn_raw%d" % gt))
+        q_view = test_view.rearrange("(p a) d -> p a d", a=8)
+        lr_raw = [None, None]
+        w_raw = [None, None]
+        lr_raw[0] = load(lr_w[0:H, :].rearrange("(a p) d -> p a d", p=P), "lr_raw0")
+        w_raw[0] = load(W[0:H, :].rearrange("(a p) d -> p a d", p=P), "w_raw0")
+
+        e_codes = const.tile([P, 2, D], U32, align_bytes=64)
+        e_scales = const.tile([P, 2, D], U8, align_bytes=64)
+        t_codes = const.tile([P, 2, D], U32, align_bytes=64)
+        t_scales = const.tile([P, 2, D], U8, align_bytes=64)
+        w_codes = const.tile([P, 2, D], U32, align_bytes=64)
+        w_scales = const.tile([P, 2, D], U8, align_bytes=64)
+        q_codes = const.tile([P, 2, T], U32, align_bytes=64)
+        q_scales = const.tile([P, 2, T], U8, align_bytes=64)
+        lrT = const.tile([P, 4 * D], F32)
+        wT = const.tile([P, 4 * D], F32)
+        qb = const.tile([P, 8, D], F32)
+        b_bc = const.tile([P, D], F32)
+        lrbs = const.tile([P, D], F32)
+
+        def quantise(grouped, codes, scales):
+            nc.vector.quantize_mx(out=codes.bitcast(FP8X4), scales=scales, in_=grouped)
+
+        for k in range(4):
+            pb = ps.tile([P, H], F32, tag="acc", name="pb")
+            nc.tensor.matmul(out=pb[:], lhsT=ones[:], rhs=zr[:, H * k:H * k + H], start=True, stop=True)
+            if k < 2:
+                nc.vector.tensor_copy(out=b_bc[:, H * k:H * k + H], in_=pb[:])
+            else:
+                nc.scalar.mul(out=lrbs[:, H * (k - 2):H * (k - 2) + H], in_=pb[:], mul=-C)
+
+        gbp = [ps.tile([P, H], F32, tag="tp", name="gbp%d" % hh) for hh in range(2)]
+        for gt in range(2):
+            for hh in range(2):
+                cols = slice(H * hh, H * hh + H)
+                ge = grp.tile([P, 4 * H], BF16, tag="grp", name="ge", align_bytes=64)
+                dst = ge[:].rearrange("p (c i t) -> p c t i", i=4, t=4)
+                src = err_raw[gt][:, :, cols].rearrange("p t (c i) -> p c t i", i=4)
+                if hh == 0:
+                    nc.vector.tensor_copy(out=dst, in_=src)
+                else:
+                    nc.scalar.copy(out=dst, in_=src)
+                quantise(ge[:], e_codes[:, gt, cols], e_scales[:, gt, cols])
+            for j in range(4):
+                for hh in range(2):
+                    nc.tensor.matmul(out=gbp[hh][:], lhsT=ones[:], rhs=err_raw[gt][:, j, H * hh:H * hh + H],
+                                     start=(gt == 0 and j == 0), stop=(gt == 1 and j == 3))
+            for g in range(2):
+                cols = slice(H * g, H * g + H)
+                gr = grp.tile([P, 4 * H], BF16, tag="grp", name="gr", align_bytes=64)
+                for u in range(2):
+                    dst = gr[:, 4 * 256 * u:4 * 256 * (u + 1)].rearrange("p (e q j) -> p q e j", e=2, j=4)
+                    src = trn_raw[gt][:, :, H * g + 256 * u:H * g + 256 * (u + 1)].rearrange(
+                        "p j (q e) -> p q e j", e=2)
+                    if g == 0:
+                        nc.vector.tensor_copy(out=dst, in_=src)
+                    else:
+                        nc.scalar.copy(out=dst, in_=src)
+                quantise(gr[:], t_codes[:, gt, cols], t_scales[:, gt, cols])
+
+        q_raw = [load(q_view[:, 4 * c:4 * c + 4, :], "q_raw%d" % c) for c in range(2)]
+        lr_raw[1] = load(lr_w[H:D, :].rearrange("(a p) d -> p a d", p=P), "lr_raw1")
+        w_raw[1] = load(W[H:D, :].rearrange("(a p) d -> p a d", p=P), "w_raw1")
+
+        for hh in range(2):
+            cols = slice(H * hh, H * hh + H)
+            nc.vector.tensor_tensor(out=lrbs[:, cols], in0=gbp[hh][:], in1=lrbs[:, cols], op=ALU.mult)
+        nc.gpsimd.tensor_tensor(out=b_bc[:], in0=lrbs[:], in1=b_bc[:], op=ALU.add)
+
+        lrT_bf = lrT[:].bitcast(BF16).rearrange("p (w o e) -> p w o e", w=4, e=2)
+        wT_bf = wT[:].bitcast(BF16).rearrange("p (w o e) -> p w o e", w=4, e=2)
+
+        def transpose_weights(raw, dstT, h):
+            for wb in range(4):
+                tp = ps.tile([P, H], F32, tag="tp", name="tp")
+                for ab in range(4):
+                    nc.tensor.transpose(tp[:, P * ab:P * ab + P],
+                                        raw[:, ab, :].bitcast(F32)[:, P * wb:P * wb + P], ident[:])
+                nc.scalar.copy(out=dstT[:, D * wb + H * h:D * wb + H * h + H], in_=tp[:])
+
+        def new_weights(h):
+            cols = slice(H * h, H * h + H)
+            transpose_weights(lr_raw[h], lrT, h)
+            tmps = []
+            for g in range(2):
+                tmp = tmpp.tile([P, 4, H], F32, tag="tmp", name="tmp")
+                tmps.append(tmp)
+                for ue in range(4):
+                    u, e = divmod(ue, 2)
+                    w0 = H * g + P * ue
+                    acc = ps.tile([P, H], F32, tag="acc", name="acc")
+                    for gt in range(2):
+                        nc.tensor.matmul_mx(out=acc[:],
+                                            lhsT=t_codes[:, gt, w0:w0 + P].bitcast(FP8X4),
+                                            lhsT_scale=t_scales[:, gt, w0:w0 + P],
+                                            rhs=e_codes[:, gt, cols].bitcast(FP8X4),
+                                            rhs_scale=e_scales[:, gt, cols],
+                                            start=(gt == 0), stop=(gt == 1))
+                    nc.vector.scalar_tensor_tensor(out=tmp[:, ue, :], in0=acc[:], scalar=-C,
+                                                   in1=lrT_bf[:, 2 * g + u, cols, e],
+                                                   op0=ALU.mult, op1=ALU.mult)
+            transpose_weights(w_raw[h], wT, h)
+            for g in range(2):
+                gw = grp.tile([P, 4 * H], BF16, tag="grp", name="gw", align_bytes=64)
+                nc.vector.tensor_tensor(out=gw[:].rearrange("p (o u e) -> p o u e", u=2, e=2),
+                                        in0=tmps[g][:].rearrange("p (u e) o -> p o u e", u=2),
+                                        in1=wT_bf[:, 2 * g:2 * g + 2, cols, :].rearrange("p u o e -> p o u e"),
+                                        op=ALU.add)
+                quantise(gw[:], w_codes[:, g, cols], w_scales[:, g, cols])
+
+        out_v = out.rearrange("(p a) d -> p a d", a=8)
+
+        def query(h):
+            cols = slice(H * h, H * h + H)
+            for a in range(8):
+                acc = ps.tile([P, H], F32, tag="acc", name="acc")
+                for g in range(2):
+                    nc.tensor.matmul_mx(out=acc[:],
+                                        lhsT=q_codes[:, g, P * a:P * a + P].bitcast(FP8X4),
+                                        lhsT_scale=q_scales[:, g, P * a:P * a + P],
+                                        rhs=w_codes[:, g, cols].bitcast(FP8X4),
+                                        rhs_scale=w_scales[:, g, cols],
+                                        start=(g == 0), stop=(g == 1))
+                nc.vector.tensor_tensor(out=qb[:, a, cols], in0=acc[:], in1=qb[:, a, cols], op=ALU.add)
+                if a % 2 == 1:
+                    nc.sync.dma_start(out=out_v[:, a - 1:a + 1, cols], in_=qb[:, a - 1:a + 1, cols])
+
+        new_weights(0)
+
+        for c in range(2):
+            gq = gqp.tile([P, 2 * 4 * H], BF16, tag="gq", name="gq", align_bytes=64)
+            gq_w = gq[:].bitcast(F32).rearrange("p (g t u) -> p g t u", g=2, u=2)
+            for a4 in range(4):
+                tp = ps.tile([P, 4, P], F32, tag="tp", name="tpq")
+                for wb in range(4):
+                    nc.tensor.transpose(tp[:, wb, :], q_raw[c][:, a4, :].bitcast(F32)[:, P * wb:P * wb + P],
+                                        ident[:])
+                nc.scalar.copy(out=gq_w[:, :, P * a4:P * a4 + P, :],
+                               in_=tp[:].rearrange("p (g u) t -> p g t u", g=2))
+            for g in range(2):
+                tc_cols = slice(H * c, H * c + H)
+                quantise(gq[:, 4 * H * g:4 * H * (g + 1)], q_codes[:, g, tc_cols], q_scales[:, g, tc_cols])
+        for h in range(2):
+            cols = slice(H * h, H * h + H)
+            for a2 in range(4):
+                c, r = divmod(2 * a2, 4)
+                nc.gpsimd.tensor_tensor(out=qb[:, 2 * a2:2 * a2 + 2, cols], in0=q_raw[c][:, r:r + 2, cols],
+                                        in1=b_bc[:, cols].unsqueeze(1).to_broadcast([P, 2, H]), op=ALU.add)
+
+        query(0)
+        new_weights(1)
+        query(1)

@@ -27,32 +27,22 @@ def tile_tttinner_pb_kernel(tc, err, train_view, test_view, W, b, lr_w, lr_b, ou
         gqp = ctx.enter_context(tc.tile_pool(name="gqp", bufs=2))
         tmpp = ctx.enter_context(tc.tile_pool(name="tmpp", bufs=2))
         ps = ctx.enter_context(tc.psum_pool(name="ps", bufs=4))
+        ctx.enter_context(tc.manual_schedule())
+
+        V = nc.vector
+        S = nc.scalar
+        G = nc.gpsimd
+        full = slice(0, D)
+
+        def hs(h):
+            return slice(H * h, H * h + H)
 
         zr = const.tile([P, 2 * D], BF16)
-        nc.vector.memset(zr[:], 0.0)
+        V.memset(zr[:], 0.0)
         ones = const.tile([P, P], BF16)
-        nc.vector.memset(ones[:], 1.0)
+        V.memset(ones[:], 1.0)
         ident = const.tile([P, P], F32)
         make_identity(nc, ident[:])
-        nc.scalar.dma_start(out=zr[0:1, 0:D], in_=b.rearrange("(o d) -> o d", o=1))
-        nc.scalar.dma_start(out=zr[0:1, D:2 * D], in_=lr_b.rearrange("(o d) -> o d", o=1))
-
-        def load(view, nm):
-            t = rawp.tile([P, 4, D], BF16, tag="raw", name=nm)
-            nc.sync.dma_start(out=t[:], in_=view)
-            return t
-
-        err_raw = []
-        trn_raw = []
-        for gt in range(2):
-            rows = slice(H * gt, H * gt + H)
-            err_raw.append(load(err[rows, :].rearrange("(p j) w -> p j w", j=4), "err_raw%d" % gt))
-            trn_raw.append(load(train_view[rows, :].rearrange("(p j) w -> p j w", j=4), "trn_raw%d" % gt))
-        q_view = test_view.rearrange("(p a) d -> p a d", a=8)
-        lr_raw = [None, None]
-        w_raw = [None, None]
-        lr_raw[0] = load(lr_w[0:H, :].rearrange("(a p) d -> p a d", p=P), "lr_raw0")
-        w_raw[0] = load(W[0:H, :].rearrange("(a p) d -> p a d", p=P), "w_raw0")
 
         e_codes = const.tile([P, 2, D], U32, align_bytes=64)
         e_scales = const.tile([P, 2, D], U8, align_bytes=64)
@@ -66,137 +56,232 @@ def tile_tttinner_pb_kernel(tc, err, train_view, test_view, W, b, lr_w, lr_b, ou
         wT = const.tile([P, 4 * D], F32)
         qb = const.tile([P, 8, D], F32)
         b_bc = const.tile([P, D], F32)
-        lrbs = const.tile([P, D], F32)
-
-        def quantise(grouped, codes, scales):
-            nc.vector.quantize_mx(out=codes.bitcast(FP8X4), scales=scales, in_=grouped)
-
-        for k in range(4):
-            pb = ps.tile([P, H], F32, tag="acc", name="pb")
-            nc.tensor.matmul(out=pb[:], lhsT=ones[:], rhs=zr[:, H * k:H * k + H], start=True, stop=True)
-            if k < 2:
-                nc.vector.tensor_copy(out=b_bc[:, H * k:H * k + H], in_=pb[:])
-            else:
-                nc.scalar.mul(out=lrbs[:, H * (k - 2):H * (k - 2) + H], in_=pb[:], mul=-C)
-
-        gbp = [ps.tile([P, H], F32, tag="tp", name="gbp%d" % hh) for hh in range(2)]
-        for gt in range(2):
-            for hh in range(2):
-                cols = slice(H * hh, H * hh + H)
-                ge = grp.tile([P, 4 * H], BF16, tag="grp", name="ge", align_bytes=64)
-                dst = ge[:].rearrange("p (c i t) -> p c t i", i=4, t=4)
-                src = err_raw[gt][:, :, cols].rearrange("p t (c i) -> p c t i", i=4)
-                if hh == 0:
-                    nc.vector.tensor_copy(out=dst, in_=src)
-                else:
-                    nc.scalar.copy(out=dst, in_=src)
-                quantise(ge[:], e_codes[:, gt, cols], e_scales[:, gt, cols])
-            for j in range(4):
-                for hh in range(2):
-                    nc.tensor.matmul(out=gbp[hh][:], lhsT=ones[:], rhs=err_raw[gt][:, j, H * hh:H * hh + H],
-                                     start=(gt == 0 and j == 0), stop=(gt == 1 and j == 3))
-            for g in range(2):
-                cols = slice(H * g, H * g + H)
-                gr = grp.tile([P, 4 * H], BF16, tag="grp", name="gr", align_bytes=64)
-                for u in range(2):
-                    dst = gr[:, 4 * 256 * u:4 * 256 * (u + 1)].rearrange("p (e q j) -> p q e j", e=2, j=4)
-                    src = trn_raw[gt][:, :, H * g + 256 * u:H * g + 256 * (u + 1)].rearrange(
-                        "p j (q e) -> p q e j", e=2)
-                    if g == 0:
-                        nc.vector.tensor_copy(out=dst, in_=src)
-                    else:
-                        nc.scalar.copy(out=dst, in_=src)
-                quantise(gr[:], t_codes[:, gt, cols], t_scales[:, gt, cols])
-
-        q_raw = [load(q_view[:, 4 * c:4 * c + 4, :], "q_raw%d" % c) for c in range(2)]
-        lr_raw[1] = load(lr_w[H:D, :].rearrange("(a p) d -> p a d", p=P), "lr_raw1")
-        w_raw[1] = load(W[H:D, :].rearrange("(a p) d -> p a d", p=P), "w_raw1")
-
-        for hh in range(2):
-            cols = slice(H * hh, H * hh + H)
-            nc.vector.tensor_tensor(out=lrbs[:, cols], in0=gbp[hh][:], in1=lrbs[:, cols], op=ALU.mult)
-        nc.gpsimd.tensor_tensor(out=b_bc[:], in0=lrbs[:], in1=b_bc[:], op=ALU.add)
-
+        lrb = const.tile([P, D], F32)
+        gbs = const.tile([P, D], F32)
         lrT_bf = lrT[:].bitcast(BF16).rearrange("p (w o e) -> p w o e", w=4, e=2)
         wT_bf = wT[:].bitcast(BF16).rearrange("p (w o e) -> p w o e", w=4, e=2)
+        q_view = test_view.rearrange("(p a) d -> p a d", a=8)
+        out_v = out.rearrange("(p a) d -> p a d", a=8)
+        raw = {}
+        grouped = {}
+        gbp = {}
+        tmps = {}
+        transposed = {"lr": lrT, "w": wT}
 
-        def transpose_weights(raw, dstT, h):
-            for wb in range(4):
+        def small_loads(queue):
+            queue.dma_start(out=zr[0:1, 0:D], in_=b.rearrange("(o d) -> o d", o=1))
+            queue.dma_start(out=zr[0:1, D:2 * D], in_=lr_b.rearrange("(o d) -> o d", o=1))
+
+        def raw_tile(nm):
+            return rawp.tile([P, 4, D], BF16, tag="raw", name=nm)
+
+        def k_rows(x, gt, cols):
+            return x[H * gt:H * gt + H, cols].rearrange("(p j) w -> p j w", j=4)
+
+        def o_rows(x, h, cols):
+            return x[hs(h), cols].rearrange("(a p) d -> p a d", p=P)
+
+        def quantise(grouped_ap, codes, scales):
+            V.quantize_mx(out=codes.bitcast(FP8X4), scales=scales, in_=grouped_ap)
+
+        def copy_on(eng, dst, src):
+            if eng is V:
+                V.tensor_copy(out=dst, in_=src)
+            else:
+                S.copy(out=dst, in_=src)
+
+        def bc(k, eng):
+            pb = ps.tile([P, H], F32, tag="acc", name="pb")
+            nc.tensor.matmul(out=pb[:], lhsT=ones[:], rhs=zr[:, H * k:H * k + H], start=True, stop=True)
+            copy_on(eng, b_bc[:, hs(k)] if k < 2 else lrb[:, hs(k - 2)], pb[:])
+
+        def rg_err(gt, h, shares):
+            ge = grp.tile([P, 4 * H], BF16, tag="grp", name="ge", align_bytes=64)
+            grouped[("e", gt, h)] = ge
+            for eng, c0, c1 in shares:
+                copy_on(eng, ge[:, 4 * c0:4 * c1].rearrange("p (c i t) -> p c t i", i=4, t=4),
+                        raw["err%d" % gt][:, :, H * h + c0:H * h + c1].rearrange("p t (c i) -> p c t i", i=4))
+
+        def q_err(gt, h):
+            quantise(grouped[("e", gt, h)][:], e_codes[:, gt, hs(h)], e_scales[:, gt, hs(h)])
+
+        def rg_trn(gt, g, engs):
+            gr = grp.tile([P, 4 * H], BF16, tag="grp", name="gr", align_bytes=64)
+            grouped[("t", gt, g)] = gr
+            for u in range(2):
+                copy_on(engs[u], gr[:, 1024 * u:1024 * (u + 1)].rearrange("p (e q j) -> p q e j", e=2, j=4),
+                        raw["trn%d" % gt][:, :, H * g + 256 * u:H * g + 256 * (u + 1)].rearrange(
+                            "p j (q e) -> p q e j", e=2))
+
+        def q_trn(gt, g):
+            quantise(grouped[("t", gt, g)][:], t_codes[:, gt, hs(g)], t_scales[:, gt, hs(g)])
+
+        def gb(h, gt):
+            if gt == 0:
+                gbp[h] = ps.tile([P, H], F32, tag="tp", name="gbp")
+            for j in range(4):
+                nc.tensor.matmul(out=gbp[h][:], lhsT=ones[:], rhs=raw["err%d" % gt][:, j, hs(h)],
+                                 start=(gt == 0 and j == 0), stop=(gt == 1 and j == 3))
+
+        def bias(h):
+            S.mul(out=gbs[:, hs(h)], in_=gbp[h][:], mul=-C)
+            G.tensor_tensor(out=gbs[:, hs(h)], in0=gbs[:, hs(h)], in1=lrb[:, hs(h)], op=ALU.mult)
+            G.tensor_tensor(out=b_bc[:, hs(h)], in0=gbs[:, hs(h)], in1=b_bc[:, hs(h)], op=ALU.add)
+
+        def t_weights(which, h, wbs):
+            src = raw["%s%d" % (which, h)]
+            tps = []
+            for wb in wbs:
                 tp = ps.tile([P, H], F32, tag="tp", name="tp")
+                tps.append(tp)
                 for ab in range(4):
                     nc.tensor.transpose(tp[:, P * ab:P * ab + P],
-                                        raw[:, ab, :].bitcast(F32)[:, P * wb:P * wb + P], ident[:])
-                nc.scalar.copy(out=dstT[:, D * wb + H * h:D * wb + H * h + H], in_=tp[:])
+                                        src[:, ab, :].bitcast(F32)[:, P * wb:P * wb + P], ident[:])
+            for wb, tp in zip(wbs, tps):
+                S.copy(out=transposed[which][:, D * wb + H * h:D * wb + H * h + H], in_=tp[:])
 
-        def new_weights(h):
-            cols = slice(H * h, H * h + H)
-            transpose_weights(lr_raw[h], lrT, h)
-            tmps = []
+        def grad(g, h, ues):
+            if ues[0] == 0:
+                tmps[(g, h)] = tmpp.tile([P, 4, H], F32, tag="tmp", name="tmp")
+            tmp = tmps[(g, h)]
+            for ue in ues:
+                u, e = divmod(ue, 2)
+                w0 = H * g + P * ue
+                acc = ps.tile([P, H], F32, tag="acc", name="acc")
+                for gt in range(2):
+                    nc.tensor.matmul_mx(out=acc[:],
+                                        lhsT=t_codes[:, gt, w0:w0 + P].bitcast(FP8X4),
+                                        lhsT_scale=t_scales[:, gt, w0:w0 + P],
+                                        rhs=e_codes[:, gt, hs(h)].bitcast(FP8X4),
+                                        rhs_scale=e_scales[:, gt, hs(h)],
+                                        start=(gt == 0), stop=(gt == 1))
+                V.scalar_tensor_tensor(out=tmp[:, ue, :], in0=acc[:], scalar=-C,
+                                       in1=lrT_bf[:, 2 * g + u, hs(h), e], op0=ALU.mult, op1=ALU.mult)
+
+        def update(g, h, eng):
+            gw = grp.tile([P, 4 * H], BF16, tag="grp", name="gw", align_bytes=64)
+            grouped[("w", g, h)] = gw
+            eng.tensor_tensor(out=gw[:].rearrange("p (o u e) -> p o u e", u=2, e=2),
+                              in0=tmps[(g, h)][:].rearrange("p (u e) o -> p o u e", u=2),
+                              in1=wT_bf[:, 2 * g:2 * g + 2, hs(h), :].rearrange("p u o e -> p o u e"),
+                              op=ALU.add)
+
+        def q_wn(g, h):
+            quantise(grouped[("w", g, h)][:], w_codes[:, g, hs(h)], w_scales[:, g, hs(h)])
+
+        def t_query(c):
+            gq = gqp.tile([P, 2 * 4 * H], BF16, tag="gq", name="gq", align_bytes=64)
+            grouped[("q", c)] = gq
+            gq_w = gq[:].bitcast(F32).rearrange("p (g t u) -> p g t u", g=2, u=2)
+            for a4 in range(4):
+                tp = ps.tile([P, 4, P], F32, tag="tp", name="tpq")
+                for wb in range(4):
+                    nc.tensor.transpose(tp[:, wb, :],
+                                        raw["q%d" % c][:, a4, :].bitcast(F32)[:, P * wb:P * wb + P], ident[:])
+                S.copy(out=gq_w[:, :, P * a4:P * a4 + P, :], in_=tp[:].rearrange("p (g u) t -> p g t u", g=2))
+
+        def q_query(c):
             for g in range(2):
-                tmp = tmpp.tile([P, 4, H], F32, tag="tmp", name="tmp")
-                tmps.append(tmp)
-                for ue in range(4):
-                    u, e = divmod(ue, 2)
-                    w0 = H * g + P * ue
-                    acc = ps.tile([P, H], F32, tag="acc", name="acc")
-                    for gt in range(2):
-                        nc.tensor.matmul_mx(out=acc[:],
-                                            lhsT=t_codes[:, gt, w0:w0 + P].bitcast(FP8X4),
-                                            lhsT_scale=t_scales[:, gt, w0:w0 + P],
-                                            rhs=e_codes[:, gt, cols].bitcast(FP8X4),
-                                            rhs_scale=e_scales[:, gt, cols],
-                                            start=(gt == 0), stop=(gt == 1))
-                    nc.vector.scalar_tensor_tensor(out=tmp[:, ue, :], in0=acc[:], scalar=-C,
-                                                   in1=lrT_bf[:, 2 * g + u, cols, e],
-                                                   op0=ALU.mult, op1=ALU.mult)
-            transpose_weights(w_raw[h], wT, h)
-            for g in range(2):
-                gw = grp.tile([P, 4 * H], BF16, tag="grp", name="gw", align_bytes=64)
-                nc.vector.tensor_tensor(out=gw[:].rearrange("p (o u e) -> p o u e", u=2, e=2),
-                                        in0=tmps[g][:].rearrange("p (u e) o -> p o u e", u=2),
-                                        in1=wT_bf[:, 2 * g:2 * g + 2, cols, :].rearrange("p u o e -> p o u e"),
-                                        op=ALU.add)
-                quantise(gw[:], w_codes[:, g, cols], w_scales[:, g, cols])
+                quantise(grouped[("q", c)][:, 4 * H * g:4 * H * (g + 1)], q_codes[:, g, hs(c)], q_scales[:, g, hs(c)])
 
-        out_v = out.rearrange("(p a) d -> p a d", a=8)
+        def resid(c, h):
+            for r in (0, 2):
+                a = 4 * c + r
+                G.tensor_tensor(out=qb[:, a:a + 2, hs(h)], in0=raw["q%d" % c][:, r:r + 2, hs(h)],
+                                in1=b_bc[:, hs(h)].unsqueeze(1).to_broadcast([P, 2, H]), op=ALU.add)
 
-        def query(h):
-            cols = slice(H * h, H * h + H)
-            for a in range(8):
+        def query(h, a_list):
+            for a in a_list:
                 acc = ps.tile([P, H], F32, tag="acc", name="acc")
                 for g in range(2):
                     nc.tensor.matmul_mx(out=acc[:],
                                         lhsT=q_codes[:, g, P * a:P * a + P].bitcast(FP8X4),
                                         lhsT_scale=q_scales[:, g, P * a:P * a + P],
-                                        rhs=w_codes[:, g, cols].bitcast(FP8X4),
-                                        rhs_scale=w_scales[:, g, cols],
+                                        rhs=w_codes[:, g, hs(h)].bitcast(FP8X4),
+                                        rhs_scale=w_scales[:, g, hs(h)],
                                         start=(g == 0), stop=(g == 1))
-                nc.vector.tensor_tensor(out=qb[:, a, cols], in0=acc[:], in1=qb[:, a, cols], op=ALU.add)
+                V.tensor_tensor(out=qb[:, a, hs(h)], in0=acc[:], in1=qb[:, a, hs(h)], op=ALU.add)
                 if a % 2 == 1:
-                    nc.sync.dma_start(out=out_v[:, a - 1:a + 1, cols], in_=qb[:, a - 1:a + 1, cols])
+                    nc.sync.dma_start(out=out_v[:, a - 1:a + 1, hs(h)], in_=qb[:, a - 1:a + 1, hs(h)])
 
-        new_weights(0)
-
-        for c in range(2):
-            gq = gqp.tile([P, 2 * 4 * H], BF16, tag="gq", name="gq", align_bytes=64)
-            gq_w = gq[:].bitcast(F32).rearrange("p (g t u) -> p g t u", g=2, u=2)
-            for a4 in range(4):
-                tp = ps.tile([P, 4, P], F32, tag="tp", name="tpq")
-                for wb in range(4):
-                    nc.tensor.transpose(tp[:, wb, :], q_raw[c][:, a4, :].bitcast(F32)[:, P * wb:P * wb + P],
-                                        ident[:])
-                nc.scalar.copy(out=gq_w[:, :, P * a4:P * a4 + P, :],
-                               in_=tp[:].rearrange("p (g u) t -> p g t u", g=2))
-            for g in range(2):
-                tc_cols = slice(H * c, H * c + H)
-                quantise(gq[:, 4 * H * g:4 * H * (g + 1)], q_codes[:, g, tc_cols], q_scales[:, g, tc_cols])
-        for h in range(2):
-            cols = slice(H * h, H * h + H)
-            for a2 in range(4):
-                c, r = divmod(2 * a2, 4)
-                nc.gpsimd.tensor_tensor(out=qb[:, 2 * a2:2 * a2 + 2, cols], in0=q_raw[c][:, r:r + 2, cols],
-                                        in1=b_bc[:, cols].unsqueeze(1).to_broadcast([P, 2, H]), op=ALU.add)
-
-        query(0)
-        new_weights(1)
-        query(1)
+        small_loads(nc.sync)
+        raw["trn0"] = raw_tile("trn0")
+        raw["trn1"] = raw_tile("trn1")
+        raw["err0"] = raw_tile("err0")
+        raw["err1"] = raw_tile("err1")
+        raw["lr0"] = raw_tile("lr0")
+        raw["w0"] = raw_tile("w0")
+        nc.sync.dma_start(out=raw["trn0"][:, :, full], in_=k_rows(train_view, 0, full))
+        nc.sync.dma_start(out=raw["err0"][:, :, hs(0)], in_=k_rows(err, 0, hs(0)))
+        nc.sync.dma_start(out=raw["trn1"][:, :, full], in_=k_rows(train_view, 1, full))
+        nc.sync.dma_start(out=raw["err1"][:, :, hs(0)], in_=k_rows(err, 1, hs(0)))
+        nc.sync.dma_start(out=raw["lr0"][:, :, hs(0)], in_=o_rows(lr_w, 0, hs(0)))
+        nc.sync.dma_start(out=raw["lr0"][:, :, hs(1)], in_=o_rows(lr_w, 0, hs(1)))
+        nc.sync.dma_start(out=raw["w0"][:, :, full], in_=o_rows(W, 0, full))
+        bc(0, V)
+        bc(1, V)
+        bc(2, S)
+        bc(3, S)
+        rg_trn(0, 0, (V, V))
+        rg_trn(0, 1, (S, S))
+        q_trn(0, 0)
+        rg_err(0, 0, ((V, 0, 512),))
+        gb(0, 0)
+        q_trn(0, 1)
+        q_err(0, 0)
+        raw["q0"] = raw_tile("q0")
+        nc.sync.dma_start(out=raw["q0"][:], in_=q_view[:, 0:4, :])
+        rg_trn(1, 0, (V, V))
+        rg_trn(1, 1, (S, S))
+        rg_err(1, 0, ((V, 0, 256), (S, 256, 512),))
+        gb(0, 1)
+        q_trn(1, 0)
+        q_trn(1, 1)
+        q_err(1, 0)
+        raw["q1"] = raw_tile("q1")
+        nc.sync.dma_start(out=raw["q1"][:], in_=q_view[:, 4:8, :])
+        nc.sync.dma_start(out=raw["err0"][:, :, hs(1)], in_=k_rows(err, 0, hs(1)))
+        nc.sync.dma_start(out=raw["err1"][:, :, hs(1)], in_=k_rows(err, 1, hs(1)))
+        bias(0)
+        t_weights("lr", 0, (0, 1, 2, 3,))
+        raw["lr1"] = raw_tile("lr1")
+        nc.sync.dma_start(out=raw["lr1"][:, :, full], in_=o_rows(lr_w, 1, full))
+        grad(0, 0, (0, 1, 2, 3,))
+        grad(1, 0, (0, 1,))
+        t_weights("w", 0, (0, 1,))
+        grad(1, 0, (2, 3,))
+        t_weights("w", 0, (2, 3,))
+        raw["w1"] = raw_tile("w1")
+        nc.sync.dma_start(out=raw["w1"][:, :, full], in_=o_rows(W, 1, full))
+        update(0, 0, V)
+        update(1, 0, V)
+        resid(0, 0)
+        t_query(0)
+        resid(1, 0)
+        t_query(1)
+        q_wn(0, 0)
+        q_wn(1, 0)
+        q_query(0)
+        q_query(1)
+        gb(1, 0)
+        gb(1, 1)
+        bias(1)
+        rg_err(0, 1, ((S, 0, 512),))
+        rg_err(1, 1, ((S, 0, 512),))
+        resid(0, 1)
+        resid(1, 1)
+        query(0, (0, 1, 2, 3,))
+        t_weights("lr", 1, (0, 1, 2, 3,))
+        q_err(0, 1)
+        q_err(1, 1)
+        query(0, (4, 5, 6, 7,))
+        grad(0, 1, (0, 1, 2, 3,))
+        grad(1, 1, (0, 1,))
+        t_weights("w", 1, (0, 1,))
+        grad(1, 1, (2, 3,))
+        t_weights("w", 1, (2, 3,))
+        update(0, 1, V)
+        update(1, 1, V)
+        q_wn(0, 1)
+        q_wn(1, 1)
+        query(1, (0, 1, 2, 3, 4, 5, 6, 7,))

@@ -32,6 +32,7 @@ def tile_tttinner_pb_kernel(tc, err, train_view, test_view, W, b, lr_w, lr_b, ou
         V = nc.vector
         S = nc.scalar
         G = nc.gpsimd
+        PE = nc.tensor
         full = slice(0, D)
 
         def hs(h):
@@ -53,33 +54,36 @@ def tile_tttinner_pb_kernel(tc, err, train_view, test_view, W, b, lr_w, lr_b, ou
         q_codes = const.tile([P, 2, T], U32, align_bytes=64)
         q_scales = const.tile([P, 2, T], U8, align_bytes=64)
         lrT = const.tile([P, 4 * D], F32)
-        wT = const.tile([P, 4 * D], F32)
         qb = const.tile([P, 8, D], F32)
         b_bc = const.tile([P, D], F32)
         lrb = const.tile([P, D], F32)
         gbs = const.tile([P, D], F32)
         lrT_bf = lrT[:].bitcast(BF16).rearrange("p (w o e) -> p w o e", w=4, e=2)
-        wT_bf = wT[:].bitcast(BF16).rearrange("p (w o e) -> p w o e", w=4, e=2)
         q_view = test_view.rearrange("(p a) d -> p a d", a=8)
         out_v = out.rearrange("(p a) d -> p a d", a=8)
         raw = {}
-        grouped = {}
-        gbp = {}
-        tmps = {}
-        transposed = {"lr": lrT, "w": wT}
+        til = {}
 
-        def small_loads(queue):
-            queue.dma_start(out=zr[0:1, 0:D], in_=b.rearrange("(o d) -> o d", o=1))
-            queue.dma_start(out=zr[0:1, D:2 * D], in_=lr_b.rearrange("(o d) -> o d", o=1))
+        def small():
+            nc.sync.dma_start(out=zr[0:1, 0:D], in_=b.rearrange("(o d) -> o d", o=1))
+            nc.sync.dma_start(out=zr[0:1, D:2 * D], in_=lr_b.rearrange("(o d) -> o d", o=1))
 
-        def raw_tile(nm):
-            return rawp.tile([P, 4, D], BF16, tag="raw", name=nm)
-
-        def k_rows(x, gt, cols):
-            return x[H * gt:H * gt + H, cols].rearrange("(p j) w -> p j w", j=4)
-
-        def o_rows(x, h, cols):
-            return x[hs(h), cols].rearrange("(a p) d -> p a d", p=P)
+        def ld(nm, cols):
+            if nm not in raw:
+                raw[nm] = rawp.tile([P, 4, D], BF16, tag="raw", name=nm)
+            kind = nm[:-1]
+            n = int(nm[-1])
+            if kind == "trn":
+                src = train_view[H * n:H * n + H, cols].rearrange("(p j) w -> p j w", j=4)
+            elif kind == "err":
+                src = err[H * n:H * n + H, cols].rearrange("(p j) w -> p j w", j=4)
+            elif kind == "lr":
+                src = lr_w[hs(n), cols].rearrange("(a p) d -> p a d", p=P)
+            elif kind == "w":
+                src = W[hs(n), cols].rearrange("(a p) d -> p a d", p=P)
+            else:
+                src = q_view[:, 4 * n:4 * n + 4, cols]
+            nc.sync.dma_start(out=raw[nm][:, :, cols], in_=src)
 
         def quantise(grouped_ap, codes, scales):
             V.quantize_mx(out=codes.bitcast(FP8X4), scales=scales, in_=grouped_ap)
@@ -90,198 +94,329 @@ def tile_tttinner_pb_kernel(tc, err, train_view, test_view, W, b, lr_w, lr_b, ou
             else:
                 S.copy(out=dst, in_=src)
 
-        def bc(k, eng):
-            pb = ps.tile([P, H], F32, tag="acc", name="pb")
-            nc.tensor.matmul(out=pb[:], lhsT=ones[:], rhs=zr[:, H * k:H * k + H], start=True, stop=True)
-            copy_on(eng, b_bc[:, hs(k)] if k < 2 else lrb[:, hs(k - 2)], pb[:])
+        def grp_tile(key):
+            if key not in til:
+                til[key] = grp.tile([P, 4 * H], BF16, tag="grp", name="grouped", align_bytes=64)
+            return til[key]
 
-        def rg_err(gt, h, shares):
-            ge = grp.tile([P, 4 * H], BF16, tag="grp", name="ge", align_bytes=64)
-            grouped[("e", gt, h)] = ge
-            for eng, c0, c1 in shares:
-                copy_on(eng, ge[:, 4 * c0:4 * c1].rearrange("p (c i t) -> p c t i", i=4, t=4),
-                        raw["err%d" % gt][:, :, H * h + c0:H * h + c1].rearrange("p t (c i) -> p c t i", i=4))
+        def bcm(k):
+            til[("pb", k)] = ps.tile([P, H], F32, tag="acc", name="pb")
+            PE.matmul(out=til[("pb", k)][:], lhsT=ones[:], rhs=zr[:, H * k:H * k + H], start=True, stop=True)
 
-        def q_err(gt, h):
-            quantise(grouped[("e", gt, h)][:], e_codes[:, gt, hs(h)], e_scales[:, gt, hs(h)])
+        def bce(k, eng):
+            copy_on(eng, b_bc[:, hs(k)] if k < 2 else lrb[:, hs(k - 2)], til[("pb", k)][:])
 
-        def rg_trn(gt, g, engs):
-            gr = grp.tile([P, 4 * H], BF16, tag="grp", name="gr", align_bytes=64)
-            grouped[("t", gt, g)] = gr
-            for u in range(2):
-                copy_on(engs[u], gr[:, 1024 * u:1024 * (u + 1)].rearrange("p (e q j) -> p q e j", e=2, j=4),
-                        raw["trn%d" % gt][:, :, H * g + 256 * u:H * g + 256 * (u + 1)].rearrange(
-                            "p j (q e) -> p q e j", e=2))
+        def rge(gt, h, c0, c1, eng):
+            ge = grp_tile(("e", gt, h))
+            copy_on(eng, ge[:, 4 * c0:4 * c1].rearrange("p (c i t) -> p c t i", i=4, t=4),
+                    raw["err%d" % gt][:, :, H * h + c0:H * h + c1].rearrange("p t (c i) -> p c t i", i=4))
 
-        def q_trn(gt, g):
-            quantise(grouped[("t", gt, g)][:], t_codes[:, gt, hs(g)], t_scales[:, gt, hs(g)])
+        def qe(gt, h):
+            quantise(til[("e", gt, h)][:], e_codes[:, gt, hs(h)], e_scales[:, gt, hs(h)])
+
+        def rgt(gt, g, u, eng):
+            gr = grp_tile(("t", gt, g))
+            copy_on(eng, gr[:, 1024 * u:1024 * (u + 1)].rearrange("p (e q j) -> p q e j", e=2, j=4),
+                    raw["trn%d" % gt][:, :, H * g + 256 * u:H * g + 256 * (u + 1)].rearrange(
+                        "p j (q e) -> p q e j", e=2))
+
+        def qt(gt, g):
+            quantise(til[("t", gt, g)][:], t_codes[:, gt, hs(g)], t_scales[:, gt, hs(g)])
 
         def gb(h, gt):
-            if gt == 0:
-                gbp[h] = ps.tile([P, H], F32, tag="tp", name="gbp")
+            if ("gb", h) not in til:
+                til[("gb", h)] = ps.tile([P, H], F32, tag="tp", name="gbp")
             for j in range(4):
-                nc.tensor.matmul(out=gbp[h][:], lhsT=ones[:], rhs=raw["err%d" % gt][:, j, hs(h)],
-                                 start=(gt == 0 and j == 0), stop=(gt == 1 and j == 3))
+                PE.matmul(out=til[("gb", h)][:], lhsT=ones[:], rhs=raw["err%d" % gt][:, j, hs(h)],
+                          start=(gt == 0 and j == 0), stop=(gt == 1 and j == 3))
 
-        def bias(h):
-            S.mul(out=gbs[:, hs(h)], in_=gbp[h][:], mul=-C)
+        def ev_gb(h):
+            S.mul(out=gbs[:, hs(h)], in_=til[("gb", h)][:], mul=-C)
+
+        def gmul(h):
             G.tensor_tensor(out=gbs[:, hs(h)], in0=gbs[:, hs(h)], in1=lrb[:, hs(h)], op=ALU.mult)
+
+        def gadd(h):
             G.tensor_tensor(out=b_bc[:, hs(h)], in0=gbs[:, hs(h)], in1=b_bc[:, hs(h)], op=ALU.add)
 
-        def t_weights(which, h, wbs):
-            src = raw["%s%d" % (which, h)]
-            tps = []
-            for wb in wbs:
-                tp = ps.tile([P, H], F32, tag="tp", name="tp")
-                tps.append(tp)
-                for ab in range(4):
-                    nc.tensor.transpose(tp[:, P * ab:P * ab + P],
-                                        src[:, ab, :].bitcast(F32)[:, P * wb:P * wb + P], ident[:])
-            for wb, tp in zip(wbs, tps):
-                S.copy(out=transposed[which][:, D * wb + H * h:D * wb + H * h + H], in_=tp[:])
+        def t_lr(h, wb):
+            tp = ps.tile([P, H], F32, tag="tp", name="tp_lr")
+            til[("lrp", h, wb)] = tp
+            for ab in range(4):
+                PE.transpose(tp[:, P * ab:P * ab + P],
+                             raw["lr%d" % h][:, ab, :].bitcast(F32)[:, P * wb:P * wb + P], ident[:])
 
-        def grad(g, h, ues):
-            if ues[0] == 0:
-                tmps[(g, h)] = tmpp.tile([P, 4, H], F32, tag="tmp", name="tmp")
-            tmp = tmps[(g, h)]
-            for ue in ues:
-                u, e = divmod(ue, 2)
-                w0 = H * g + P * ue
-                acc = ps.tile([P, H], F32, tag="acc", name="acc")
-                for gt in range(2):
-                    nc.tensor.matmul_mx(out=acc[:],
-                                        lhsT=t_codes[:, gt, w0:w0 + P].bitcast(FP8X4),
-                                        lhsT_scale=t_scales[:, gt, w0:w0 + P],
-                                        rhs=e_codes[:, gt, hs(h)].bitcast(FP8X4),
-                                        rhs_scale=e_scales[:, gt, hs(h)],
-                                        start=(gt == 0), stop=(gt == 1))
-                V.scalar_tensor_tensor(out=tmp[:, ue, :], in0=acc[:], scalar=-C,
-                                       in1=lrT_bf[:, 2 * g + u, hs(h), e], op0=ALU.mult, op1=ALU.mult)
+        def ev_lr(h, wb):
+            S.copy(out=lrT[:, D * wb + H * h:D * wb + H * h + H], in_=til[("lrp", h, wb)][:])
 
-        def update(g, h, eng):
-            gw = grp.tile([P, 4 * H], BF16, tag="grp", name="gw", align_bytes=64)
-            grouped[("w", g, h)] = gw
-            eng.tensor_tensor(out=gw[:].rearrange("p (o u e) -> p o u e", u=2, e=2),
-                              in0=tmps[(g, h)][:].rearrange("p (u e) o -> p o u e", u=2),
-                              in1=wT_bf[:, 2 * g:2 * g + 2, hs(h), :].rearrange("p u o e -> p o u e"),
-                              op=ALU.add)
+        def mx1(g, h, ue):
+            w0 = H * g + P * ue
+            acc = ps.tile([P, H], F32, tag="acc", name="acc1")
+            til[("a1", g, h, ue)] = acc
+            for gt in range(2):
+                PE.matmul_mx(out=acc[:],
+                             lhsT=t_codes[:, gt, w0:w0 + P].bitcast(FP8X4), lhsT_scale=t_scales[:, gt, w0:w0 + P],
+                             rhs=e_codes[:, gt, hs(h)].bitcast(FP8X4), rhs_scale=e_scales[:, gt, hs(h)],
+                             start=(gt == 0), stop=(gt == 1))
 
-        def q_wn(g, h):
-            quantise(grouped[("w", g, h)][:], w_codes[:, g, hs(h)], w_scales[:, g, hs(h)])
+        def p1(g, h, ue):
+            if ("tmp", g, h) not in til:
+                til[("tmp", g, h)] = tmpp.tile([P, 4, H], F32, tag="tmp", name="tmp")
+            u, e = divmod(ue, 2)
+            V.scalar_tensor_tensor(out=til[("tmp", g, h)][:, ue, :], in0=til[("a1", g, h, ue)][:], scalar=-C,
+                                   in1=lrT_bf[:, 2 * g + u, hs(h), e], op0=ALU.mult, op1=ALU.mult)
 
-        def t_query(c):
-            gq = gqp.tile([P, 2 * 4 * H], BF16, tag="gq", name="gq", align_bytes=64)
-            grouped[("q", c)] = gq
-            gq_w = gq[:].bitcast(F32).rearrange("p (g t u) -> p g t u", g=2, u=2)
-            for a4 in range(4):
-                tp = ps.tile([P, 4, P], F32, tag="tp", name="tpq")
-                for wb in range(4):
-                    nc.tensor.transpose(tp[:, wb, :],
-                                        raw["q%d" % c][:, a4, :].bitcast(F32)[:, P * wb:P * wb + P], ident[:])
-                S.copy(out=gq_w[:, :, P * a4:P * a4 + P, :], in_=tp[:].rearrange("p (g u) t -> p g t u", g=2))
+        def t_w(g, h, oq):
+            tp = ps.tile([P, H], F32, tag="tp", name="tp_w")
+            til[("wp", g, h, oq)] = tp
+            for u in range(2):
+                for k in range(2):
+                    wb = 2 * g + u
+                    PE.transpose(tp[:, 256 * u + P * k:256 * u + P * k + P],
+                                 raw["w%d" % h][:, 2 * oq + k, :].bitcast(F32)[:, P * wb:P * wb + P], ident[:])
 
-        def q_query(c):
+        def p2(g, h, oq):
+            gw = grp_tile(("w", g, h))
+            o0 = 256 * oq
+            V.tensor_tensor(out=gw[:, 4 * o0:4 * o0 + 1024].rearrange("p (o u e) -> p o u e", u=2, e=2),
+                            in0=til[("tmp", g, h)][:, :, o0:o0 + 256].rearrange("p (u e) o -> p o u e", u=2),
+                            in1=til[("wp", g, h, oq)][:].bitcast(BF16).rearrange("p (u o e) -> p o u e", u=2, e=2),
+                            op=ALU.add)
+
+        def qw(g, h):
+            quantise(til[("w", g, h)][:], w_codes[:, g, hs(h)], w_scales[:, g, hs(h)])
+
+        def t_q(c, a4):
+            tp = ps.tile([P, 4, P], F32, tag="tp", name="tp_q")
+            til[("qp", c, a4)] = tp
+            for wb in range(4):
+                PE.transpose(tp[:, wb, :], raw["q%d" % c][:, a4, :].bitcast(F32)[:, P * wb:P * wb + P], ident[:])
+
+        def ev_q(c, a4):
+            if ("gq", c) not in til:
+                til[("gq", c)] = gqp.tile([P, 2 * 4 * H], BF16, tag="gq", name="gq", align_bytes=64)
+            gq_w = til[("gq", c)][:].bitcast(F32).rearrange("p (g t u) -> p g t u", g=2, u=2)
+            S.copy(out=gq_w[:, :, P * a4:P * a4 + P, :],
+                   in_=til[("qp", c, a4)][:].rearrange("p (g u) t -> p g t u", g=2))
+
+        def qq(c, g):
+            quantise(til[("gq", c)][:, 4 * H * g:4 * H * (g + 1)], q_codes[:, g, hs(c)], q_scales[:, g, hs(c)])
+
+        def resid(a, h):
+            G.tensor_tensor(out=qb[:, a, hs(h)], in0=raw["q%d" % (a // 4)][:, a % 4, hs(h)], in1=b_bc[:, hs(h)],
+                            op=ALU.add)
+
+        def mx2(h, a):
+            acc = ps.tile([P, H], F32, tag="acc", name="acc2")
+            til[("a2", h, a)] = acc
             for g in range(2):
-                quantise(grouped[("q", c)][:, 4 * H * g:4 * H * (g + 1)], q_codes[:, g, hs(c)], q_scales[:, g, hs(c)])
+                PE.matmul_mx(out=acc[:],
+                             lhsT=q_codes[:, g, P * a:P * a + P].bitcast(FP8X4),
+                             lhsT_scale=q_scales[:, g, P * a:P * a + P],
+                             rhs=w_codes[:, g, hs(h)].bitcast(FP8X4), rhs_scale=w_scales[:, g, hs(h)],
+                             start=(g == 0), stop=(g == 1))
 
-        def resid(c, h):
-            for r in (0, 2):
-                a = 4 * c + r
-                G.tensor_tensor(out=qb[:, a:a + 2, hs(h)], in0=raw["q%d" % c][:, r:r + 2, hs(h)],
-                                in1=b_bc[:, hs(h)].unsqueeze(1).to_broadcast([P, 2, H]), op=ALU.add)
+        def e1(h, a):
+            V.tensor_tensor(out=qb[:, a, hs(h)], in0=til[("a2", h, a)][:], in1=qb[:, a, hs(h)], op=ALU.add)
 
-        def query(h, a_list):
-            for a in a_list:
-                acc = ps.tile([P, H], F32, tag="acc", name="acc")
-                for g in range(2):
-                    nc.tensor.matmul_mx(out=acc[:],
-                                        lhsT=q_codes[:, g, P * a:P * a + P].bitcast(FP8X4),
-                                        lhsT_scale=q_scales[:, g, P * a:P * a + P],
-                                        rhs=w_codes[:, g, hs(h)].bitcast(FP8X4),
-                                        rhs_scale=w_scales[:, g, hs(h)],
-                                        start=(g == 0), stop=(g == 1))
-                V.tensor_tensor(out=qb[:, a, hs(h)], in0=acc[:], in1=qb[:, a, hs(h)], op=ALU.add)
-                if a % 2 == 1:
-                    nc.sync.dma_start(out=out_v[:, a - 1:a + 1, hs(h)], in_=qb[:, a - 1:a + 1, hs(h)])
+        def st(h, a, n):
+            nc.sync.dma_start(out=out_v[:, a:a + n, hs(h)], in_=qb[:, a:a + n, hs(h)])
 
-        small_loads(nc.sync)
-        raw["trn0"] = raw_tile("trn0")
-        raw["trn1"] = raw_tile("trn1")
-        raw["err0"] = raw_tile("err0")
-        raw["err1"] = raw_tile("err1")
-        raw["lr0"] = raw_tile("lr0")
-        raw["w0"] = raw_tile("w0")
-        nc.sync.dma_start(out=raw["trn0"][:, :, full], in_=k_rows(train_view, 0, full))
-        nc.sync.dma_start(out=raw["err0"][:, :, hs(0)], in_=k_rows(err, 0, hs(0)))
-        nc.sync.dma_start(out=raw["trn1"][:, :, full], in_=k_rows(train_view, 1, full))
-        nc.sync.dma_start(out=raw["err1"][:, :, hs(0)], in_=k_rows(err, 1, hs(0)))
-        nc.sync.dma_start(out=raw["lr0"][:, :, hs(0)], in_=o_rows(lr_w, 0, hs(0)))
-        nc.sync.dma_start(out=raw["lr0"][:, :, hs(1)], in_=o_rows(lr_w, 0, hs(1)))
-        nc.sync.dma_start(out=raw["w0"][:, :, full], in_=o_rows(W, 0, full))
-        bc(0, V)
-        bc(1, V)
-        bc(2, S)
-        bc(3, S)
-        rg_trn(0, 0, (V, V))
-        rg_trn(0, 1, (S, S))
-        q_trn(0, 0)
-        rg_err(0, 0, ((V, 0, 512),))
+        small()
+        ld("trn0", full)
+        ld("err0", hs(0))
+        ld("trn1", full)
+        ld("err1", hs(0))
+        ld("lr0", hs(0))
+        ld("lr0", hs(1))
+        ld("w0", full)
+        bcm(0)
+        bcm(1)
+        bcm(2)
+        bcm(3)
+        bce(0, V)
+        bce(1, V)
+        bce(2, S)
+        bce(3, S)
+        rgt(0, 0, 0, V)
+        rgt(0, 0, 1, V)
+        rgt(0, 1, 0, S)
+        rgt(0, 1, 1, S)
+        qt(0, 0)
+        rge(0, 0, 0, 512, V)
         gb(0, 0)
-        q_trn(0, 1)
-        q_err(0, 0)
-        raw["q0"] = raw_tile("q0")
-        nc.sync.dma_start(out=raw["q0"][:], in_=q_view[:, 0:4, :])
-        rg_trn(1, 0, (V, V))
-        rg_trn(1, 1, (S, S))
-        rg_err(1, 0, ((V, 0, 256), (S, 256, 512),))
+        qt(0, 1)
+        qe(0, 0)
+        ld("q0", full)
+        rgt(1, 0, 0, V)
+        rgt(1, 0, 1, V)
+        rgt(1, 1, 0, S)
+        rgt(1, 1, 1, S)
+        rge(1, 0, 0, 256, V)
+        rge(1, 0, 256, 512, S)
         gb(0, 1)
-        q_trn(1, 0)
-        q_trn(1, 1)
-        q_err(1, 0)
-        raw["q1"] = raw_tile("q1")
-        nc.sync.dma_start(out=raw["q1"][:], in_=q_view[:, 4:8, :])
-        nc.sync.dma_start(out=raw["err0"][:, :, hs(1)], in_=k_rows(err, 0, hs(1)))
-        nc.sync.dma_start(out=raw["err1"][:, :, hs(1)], in_=k_rows(err, 1, hs(1)))
-        bias(0)
-        t_weights("lr", 0, (0, 1, 2, 3,))
-        raw["lr1"] = raw_tile("lr1")
-        nc.sync.dma_start(out=raw["lr1"][:, :, full], in_=o_rows(lr_w, 1, full))
-        grad(0, 0, (0, 1, 2, 3,))
-        grad(1, 0, (0, 1,))
-        t_weights("w", 0, (0, 1,))
-        grad(1, 0, (2, 3,))
-        t_weights("w", 0, (2, 3,))
-        raw["w1"] = raw_tile("w1")
-        nc.sync.dma_start(out=raw["w1"][:, :, full], in_=o_rows(W, 1, full))
-        update(0, 0, V)
-        update(1, 0, V)
+        qt(1, 0)
+        qt(1, 1)
+        qe(1, 0)
+        ld("q1", full)
+        ld("err0", hs(1))
+        ld("err1", hs(1))
+        ev_gb(0)
+        gmul(0)
+        gadd(0)
+        t_lr(0, 0)
+        t_lr(0, 1)
+        t_lr(0, 2)
+        t_lr(0, 3)
+        ev_lr(0, 0)
+        ev_lr(0, 1)
+        ev_lr(0, 2)
+        ev_lr(0, 3)
+        ld("lr1", full)
+        mx1(0, 0, 0)
+        p1(0, 0, 0)
+        mx1(0, 0, 1)
+        p1(0, 0, 1)
+        mx1(0, 0, 2)
+        p1(0, 0, 2)
+        mx1(0, 0, 3)
+        p1(0, 0, 3)
+        t_w(0, 0, 0)
+        t_w(0, 0, 1)
+        mx1(1, 0, 0)
+        mx1(1, 0, 1)
+        p2(0, 0, 0)
+        p2(0, 0, 1)
+        p1(1, 0, 0)
+        p1(1, 0, 1)
+        mx1(1, 0, 2)
+        p1(1, 0, 2)
+        mx1(1, 0, 3)
+        p1(1, 0, 3)
+        t_w(1, 0, 0)
+        t_w(1, 0, 1)
+        p2(1, 0, 0)
+        p2(1, 0, 1)
+        ld("w1", full)
         resid(0, 0)
-        t_query(0)
         resid(1, 0)
-        t_query(1)
-        q_wn(0, 0)
-        q_wn(1, 0)
-        q_query(0)
-        q_query(1)
+        resid(2, 0)
+        resid(3, 0)
+        resid(4, 0)
+        resid(5, 0)
+        resid(6, 0)
+        resid(7, 0)
+        t_q(0, 0)
+        ev_q(0, 0)
+        t_q(0, 1)
+        ev_q(0, 1)
+        t_q(0, 2)
+        ev_q(0, 2)
+        t_q(0, 3)
+        ev_q(0, 3)
+        t_q(1, 0)
+        ev_q(1, 0)
+        t_q(1, 1)
+        ev_q(1, 1)
+        t_q(1, 2)
+        ev_q(1, 2)
+        t_q(1, 3)
+        ev_q(1, 3)
+        qw(0, 0)
+        qw(1, 0)
+        qq(0, 0)
+        qq(0, 1)
+        qq(1, 0)
+        qq(1, 1)
         gb(1, 0)
         gb(1, 1)
-        bias(1)
-        rg_err(0, 1, ((S, 0, 512),))
-        rg_err(1, 1, ((S, 0, 512),))
+        ev_gb(1)
+        gmul(1)
+        gadd(1)
+        rge(0, 1, 0, 512, S)
+        rge(1, 1, 0, 512, S)
         resid(0, 1)
         resid(1, 1)
-        query(0, (0, 1, 2, 3,))
-        t_weights("lr", 1, (0, 1, 2, 3,))
-        q_err(0, 1)
-        q_err(1, 1)
-        query(0, (4, 5, 6, 7,))
-        grad(0, 1, (0, 1, 2, 3,))
-        grad(1, 1, (0, 1,))
-        t_weights("w", 1, (0, 1,))
-        grad(1, 1, (2, 3,))
-        t_weights("w", 1, (2, 3,))
-        update(0, 1, V)
-        update(1, 1, V)
-        q_wn(0, 1)
-        q_wn(1, 1)
-        query(1, (0, 1, 2, 3, 4, 5, 6, 7,))
+        resid(2, 1)
+        resid(3, 1)
+        resid(4, 1)
+        resid(5, 1)
+        resid(6, 1)
+        resid(7, 1)
+        mx2(0, 0)
+        e1(0, 0)
+        mx2(0, 1)
+        e1(0, 1)
+        st(0, 0, 2)
+        mx2(0, 2)
+        e1(0, 2)
+        mx2(0, 3)
+        e1(0, 3)
+        st(0, 2, 2)
+        t_lr(1, 0)
+        t_lr(1, 1)
+        t_lr(1, 2)
+        t_lr(1, 3)
+        ev_lr(1, 0)
+        ev_lr(1, 1)
+        ev_lr(1, 2)
+        ev_lr(1, 3)
+        qe(0, 1)
+        qe(1, 1)
+        mx2(0, 4)
+        e1(0, 4)
+        mx2(0, 5)
+        e1(0, 5)
+        st(0, 4, 2)
+        mx2(0, 6)
+        e1(0, 6)
+        mx2(0, 7)
+        e1(0, 7)
+        st(0, 6, 2)
+        mx1(0, 1, 0)
+        p1(0, 1, 0)
+        mx1(0, 1, 1)
+        p1(0, 1, 1)
+        mx1(0, 1, 2)
+        p1(0, 1, 2)
+        mx1(0, 1, 3)
+        p1(0, 1, 3)
+        t_w(0, 1, 0)
+        t_w(0, 1, 1)
+        mx1(1, 1, 0)
+        mx1(1, 1, 1)
+        p2(0, 1, 0)
+        p2(0, 1, 1)
+        p1(1, 1, 0)
+        p1(1, 1, 1)
+        mx1(1, 1, 2)
+        p1(1, 1, 2)
+        mx1(1, 1, 3)
+        p1(1, 1, 3)
+        t_w(1, 1, 0)
+        t_w(1, 1, 1)
+        p2(1, 1, 0)
+        p2(1, 1, 1)
+        qw(0, 1)
+        qw(1, 1)
+        mx2(1, 0)
+        e1(1, 0)
+        mx2(1, 1)
+        e1(1, 1)
+        st(1, 0, 2)
+        mx2(1, 2)
+        e1(1, 2)
+        mx2(1, 3)
+        e1(1, 3)
+        st(1, 2, 2)
+        mx2(1, 4)
+        e1(1, 4)
+        mx2(1, 5)
+        e1(1, 5)
+        st(1, 4, 2)
+        mx2(1, 6)
+        e1(1, 6)
+        st(1, 6, 1)
+        mx2(1, 7)
+        e1(1, 7)
+        st(1, 7, 1)

@@ -25,7 +25,7 @@ def tile_tttinner_pb_kernel(tc, err, train_view, test_view, W, b, lr_w, lr_b, ou
         rawp = ctx.enter_context(tc.tile_pool(name="rawp", bufs=6))
         grp = ctx.enter_context(tc.tile_pool(name="grp", bufs=6))
         gqp = ctx.enter_context(tc.tile_pool(name="gqp", bufs=2))
-        tmpp = ctx.enter_context(tc.tile_pool(name="tmpp", bufs=2))
+        tmpp = ctx.enter_context(tc.tile_pool(name="tmpp", bufs=4))
         ps = ctx.enter_context(tc.psum_pool(name="ps", bufs=4))
         ctx.enter_context(tc.manual_schedule())
 
@@ -38,12 +38,14 @@ def tile_tttinner_pb_kernel(tc, err, train_view, test_view, W, b, lr_w, lr_b, ou
         def hs(h):
             return slice(H * h, H * h + H)
 
-        zr = const.tile([P, 2 * D], BF16)
-        V.memset(zr[:], 0.0)
-        ones = const.tile([P, P], BF16)
+        zb = const.tile([P, P], BF16)
+        V.memset(zb[:], 0.0)
+        ones = const.tile([P, 32], BF16)
         V.memset(ones[:], 1.0)
         ident = const.tile([P, P], F32)
         make_identity(nc, ident[:])
+        ident_bf = const.tile([P, P], BF16)
+        make_identity(nc, ident_bf[:])
 
         e_codes = const.tile([P, 2, D], U32, align_bytes=64)
         e_scales = const.tile([P, 2, D], U8, align_bytes=64)
@@ -55,18 +57,18 @@ def tile_tttinner_pb_kernel(tc, err, train_view, test_view, W, b, lr_w, lr_b, ou
         q_scales = const.tile([P, 2, T], U8, align_bytes=64)
         lrT = const.tile([P, 4 * D], F32)
         qb = const.tile([P, 8, D], F32)
-        b_bc = const.tile([P, D], F32)
-        lrb = const.tile([P, D], F32)
-        gbs = const.tile([P, D], F32)
+        bb = const.tile([P, D], F32)
+        bl = const.tile([P, 16], F32)
+        bn_col = const.tile([P, 8], F32)
         lrT_bf = lrT[:].bitcast(BF16).rearrange("p (w o e) -> p w o e", w=4, e=2)
         q_view = test_view.rearrange("(p a) d -> p a d", a=8)
         out_v = out.rearrange("(p a) d -> p a d", a=8)
         raw = {}
         til = {}
 
-        def small():
-            nc.sync.dma_start(out=zr[0:1, 0:D], in_=b.rearrange("(o d) -> o d", o=1))
-            nc.sync.dma_start(out=zr[0:1, D:2 * D], in_=lr_b.rearrange("(o d) -> o d", o=1))
+        def small2():
+            nc.sync.dma_start(out=zb[0:8, :], in_=b.rearrange("(r c) -> r c", r=8))
+            nc.sync.dma_start(out=zb[8:16, :], in_=lr_b.rearrange("(r c) -> r c", r=8))
 
         def ld(nm, cols):
             if nm not in raw:
@@ -99,12 +101,38 @@ def tile_tttinner_pb_kernel(tc, err, train_view, test_view, W, b, lr_w, lr_b, ou
                 til[key] = grp.tile([P, 4 * H], BF16, tag="grp", name="grouped", align_bytes=64)
             return til[key]
 
-        def bcm(k):
-            til[("pb", k)] = ps.tile([P, H], F32, tag="acc", name="pb")
-            PE.matmul(out=til[("pb", k)][:], lhsT=ones[:], rhs=zr[:, H * k:H * k + H], start=True, stop=True)
+        def t_b():
+            til["tpb"] = ps.tile([P, P], BF16, tag="tp", name="tp_b")
+            PE.transpose(til["tpb"][:], zb[:], ident_bf[:])
 
-        def bce(k, eng):
-            copy_on(eng, b_bc[:, hs(k)] if k < 2 else lrb[:, hs(k - 2)], til[("pb", k)][:])
+        def ev_b():
+            V.tensor_copy(out=bl[:], in_=til["tpb"][:, 0:16])
+
+        def gbc(h):
+            gcp = ps.tile([P, 4, 32], F32, tag="tp", name="gcp")
+            til[("gc", h)] = gcp
+            for k in range(4):
+                o0 = H * h + P * k
+                for r in range(8):
+                    PE.matmul(out=gcp[:, k, :], lhsT=raw["err%d" % (r // 4)][:, r % 4, o0:o0 + P], rhs=ones[:],
+                              start=(r == 0), stop=(r == 7))
+
+        def bn(h):
+            sl = slice(4 * h, 4 * h + 4)
+            V.scalar_tensor_tensor(out=bn_col[:, sl], in0=til[("gc", h)][:, :, 0], scalar=-C,
+                                   in1=bl[:, 8 + 4 * h:12 + 4 * h], op0=ALU.mult, op1=ALU.mult)
+            V.tensor_tensor(out=bn_col[:, sl], in0=bn_col[:, sl], in1=bl[:, sl], op=ALU.add)
+
+        def bbm(h):
+            bbp = ps.tile([P, H], F32, tag="tp", name="bbp")
+            til[("bbp", h)] = bbp
+            for k in range(4):
+                PE.matmul(out=bbp[:, P * k:P * k + P],
+                          lhsT=bn_col[:, 4 * h + k:4 * h + k + 1].to_broadcast([P, P]), rhs=ident[:],
+                          start=True, stop=True)
+
+        def ev_bb(h):
+            S.copy(out=bb[:, hs(h)], in_=til[("bbp", h)][:])
 
         def rge(gt, h, c0, c1, eng):
             ge = grp_tile(("e", gt, h))
@@ -123,22 +151,6 @@ def tile_tttinner_pb_kernel(tc, err, train_view, test_view, W, b, lr_w, lr_b, ou
         def qt(gt, g):
             quantise(til[("t", gt, g)][:], t_codes[:, gt, hs(g)], t_scales[:, gt, hs(g)])
 
-        def gb(h, gt):
-            if ("gb", h) not in til:
-                til[("gb", h)] = ps.tile([P, H], F32, tag="tp", name="gbp")
-            for j in range(4):
-                PE.matmul(out=til[("gb", h)][:], lhsT=ones[:], rhs=raw["err%d" % gt][:, j, hs(h)],
-                          start=(gt == 0 and j == 0), stop=(gt == 1 and j == 3))
-
-        def ev_gb(h):
-            S.mul(out=gbs[:, hs(h)], in_=til[("gb", h)][:], mul=-C)
-
-        def gmul(h):
-            G.tensor_tensor(out=gbs[:, hs(h)], in0=gbs[:, hs(h)], in1=lrb[:, hs(h)], op=ALU.mult)
-
-        def gadd(h):
-            G.tensor_tensor(out=b_bc[:, hs(h)], in0=gbs[:, hs(h)], in1=b_bc[:, hs(h)], op=ALU.add)
-
         def t_lr(h, wb):
             tp = ps.tile([P, H], F32, tag="tp", name="tp_lr")
             til[("lrp", h, wb)] = tp
@@ -149,38 +161,43 @@ def tile_tttinner_pb_kernel(tc, err, train_view, test_view, W, b, lr_w, lr_b, ou
         def ev_lr(h, wb):
             S.copy(out=lrT[:, D * wb + H * h:D * wb + H * h + H], in_=til[("lrp", h, wb)][:])
 
-        def mx1(g, h, ue):
-            w0 = H * g + P * ue
+        def mx1b(g, u, oq):
             acc = ps.tile([P, H], F32, tag="acc", name="acc1")
-            til[("a1", g, h, ue)] = acc
-            for gt in range(2):
-                PE.matmul_mx(out=acc[:],
-                             lhsT=t_codes[:, gt, w0:w0 + P].bitcast(FP8X4), lhsT_scale=t_scales[:, gt, w0:w0 + P],
-                             rhs=e_codes[:, gt, hs(h)].bitcast(FP8X4), rhs_scale=e_scales[:, gt, hs(h)],
-                             start=(gt == 0), stop=(gt == 1))
+            til[("a1", g, u, oq)] = acc
+            oc = slice(256 * oq, 256 * oq + 256)
+            for e in range(2):
+                w0 = H * g + 256 * u + P * e
+                for gt in range(2):
+                    PE.matmul_mx(out=acc[:, 256 * e:256 * e + 256],
+                                 lhsT=t_codes[:, gt, w0:w0 + P].bitcast(FP8X4),
+                                 lhsT_scale=t_scales[:, gt, w0:w0 + P],
+                                 rhs=e_codes[:, gt, oc].bitcast(FP8X4), rhs_scale=e_scales[:, gt, oc],
+                                 start=(gt == 0), stop=(gt == 1))
 
-        def p1(g, h, ue):
-            if ("tmp", g, h) not in til:
-                til[("tmp", g, h)] = tmpp.tile([P, 4, H], F32, tag="tmp", name="tmp")
-            u, e = divmod(ue, 2)
-            V.scalar_tensor_tensor(out=til[("tmp", g, h)][:, ue, :], in0=til[("a1", g, h, ue)][:], scalar=-C,
-                                   in1=lrT_bf[:, 2 * g + u, hs(h), e], op0=ALU.mult, op1=ALU.mult)
+        def p1b(g, u, oq):
+            if ("tmp", g, oq) not in til:
+                til[("tmp", g, oq)] = tmpp.tile([P, 2, H], F32, tag="tmp", name="tmp")
+            V.scalar_tensor_tensor(out=til[("tmp", g, oq)][:, u, :].rearrange("p (o e) -> p o e", e=2),
+                                   in0=til[("a1", g, u, oq)][:].rearrange("p (e o) -> p o e", e=2), scalar=-C,
+                                   in1=lrT_bf[:, 2 * g + u, 256 * oq:256 * oq + 256, :],
+                                   op0=ALU.mult, op1=ALU.mult)
 
-        def t_w(g, h, oq):
+        def t_wb(g, oq):
             tp = ps.tile([P, H], F32, tag="tp", name="tp_w")
-            til[("wp", g, h, oq)] = tp
+            til[("wp", g, oq)] = tp
             for u in range(2):
                 for k in range(2):
                     wb = 2 * g + u
                     PE.transpose(tp[:, 256 * u + P * k:256 * u + P * k + P],
-                                 raw["w%d" % h][:, 2 * oq + k, :].bitcast(F32)[:, P * wb:P * wb + P], ident[:])
+                                 raw["w%d" % (oq // 2)][:, 2 * (oq % 2) + k, :].bitcast(F32)[:, P * wb:P * wb + P],
+                                 ident[:])
 
-        def p2(g, h, oq):
-            gw = grp_tile(("w", g, h))
-            o0 = 256 * oq
-            V.tensor_tensor(out=gw[:, 4 * o0:4 * o0 + 1024].rearrange("p (o u e) -> p o u e", u=2, e=2),
-                            in0=til[("tmp", g, h)][:, :, o0:o0 + 256].rearrange("p (u e) o -> p o u e", u=2),
-                            in1=til[("wp", g, h, oq)][:].bitcast(BF16).rearrange("p (u o e) -> p o u e", u=2, e=2),
+        def p2b(g, oq):
+            gw = grp_tile(("w", g, oq // 2))
+            c0 = 1024 * (oq % 2)
+            V.tensor_tensor(out=gw[:, c0:c0 + 1024].rearrange("p (o u e) -> p o u e", u=2, e=2),
+                            in0=til[("tmp", g, oq)][:].rearrange("p u (o e) -> p o u e", e=2),
+                            in1=til[("wp", g, oq)][:].bitcast(BF16).rearrange("p (u o e) -> p o u e", u=2, e=2),
                             op=ALU.add)
 
         def qw(g, h):
@@ -203,7 +220,7 @@ def tile_tttinner_pb_kernel(tc, err, train_view, test_view, W, b, lr_w, lr_b, ou
             quantise(til[("gq", c)][:, 4 * H * g:4 * H * (g + 1)], q_codes[:, g, hs(c)], q_scales[:, g, hs(c)])
 
         def resid(a, h):
-            G.tensor_tensor(out=qb[:, a, hs(h)], in0=raw["q%d" % (a // 4)][:, a % 4, hs(h)], in1=b_bc[:, hs(h)],
+            G.tensor_tensor(out=qb[:, a, hs(h)], in0=raw["q%d" % (a // 4)][:, a % 4, hs(h)], in1=bb[:, hs(h)],
                             op=ALU.add)
 
         def mx2(h, a):
@@ -222,201 +239,193 @@ def tile_tttinner_pb_kernel(tc, err, train_view, test_view, W, b, lr_w, lr_b, ou
         def st(h, a, n):
             nc.sync.dma_start(out=out_v[:, a:a + n, hs(h)], in_=qb[:, a:a + n, hs(h)])
 
-        small()
         ld("trn0", full)
+        small2()
         ld("err0", hs(0))
         ld("trn1", full)
         ld("err1", hs(0))
         ld("lr0", hs(0))
         ld("lr0", hs(1))
         ld("w0", full)
-        bcm(0)
-        bcm(1)
-        bcm(2)
-        bcm(3)
-        bce(0, V)
-        bce(1, V)
-        bce(2, S)
-        bce(3, S)
         rgt(0, 0, 0, V)
-        rgt(0, 0, 1, V)
         rgt(0, 1, 0, S)
+        t_b()
+        rgt(0, 0, 1, V)
         rgt(0, 1, 1, S)
+        gbc(0)
         qt(0, 0)
         rge(0, 0, 0, 512, V)
-        gb(0, 0)
-        qt(0, 1)
-        qe(0, 0)
         ld("q0", full)
-        rgt(1, 0, 0, V)
-        rgt(1, 0, 1, V)
+        qt(0, 1)
         rgt(1, 1, 0, S)
+        qe(0, 0)
+        rgt(1, 0, 0, V)
         rgt(1, 1, 1, S)
-        rge(1, 0, 0, 256, V)
+        rgt(1, 0, 1, V)
+        ev_b()
         rge(1, 0, 256, 512, S)
-        gb(0, 1)
-        qt(1, 0)
-        qt(1, 1)
-        qe(1, 0)
         ld("q1", full)
+        qt(1, 1)
         ld("err0", hs(1))
-        ld("err1", hs(1))
-        ev_gb(0)
-        gmul(0)
-        gadd(0)
         t_lr(0, 0)
+        ld("err1", hs(1))
         t_lr(0, 1)
-        t_lr(0, 2)
-        t_lr(0, 3)
+        bn(0)
+        rge(1, 0, 0, 256, V)
         ev_lr(0, 0)
+        t_lr(0, 2)
+        qt(1, 0)
+        bbm(0)
         ev_lr(0, 1)
-        ev_lr(0, 2)
-        ev_lr(0, 3)
+        qe(1, 0)
+        t_lr(0, 3)
+        ev_bb(0)
+        mx1b(0, 0, 0)
         ld("lr1", full)
-        mx1(0, 0, 0)
-        p1(0, 0, 0)
-        mx1(0, 0, 1)
-        p1(0, 0, 1)
-        mx1(0, 0, 2)
-        p1(0, 0, 2)
-        mx1(0, 0, 3)
-        p1(0, 0, 3)
-        t_w(0, 0, 0)
-        t_w(0, 0, 1)
-        mx1(1, 0, 0)
-        mx1(1, 0, 1)
-        p2(0, 0, 0)
-        p2(0, 0, 1)
-        p1(1, 0, 0)
-        p1(1, 0, 1)
-        mx1(1, 0, 2)
-        p1(1, 0, 2)
-        mx1(1, 0, 3)
-        p1(1, 0, 3)
-        t_w(1, 0, 0)
-        t_w(1, 0, 1)
-        p2(1, 0, 0)
-        p2(1, 0, 1)
-        ld("w1", full)
+        ev_lr(0, 2)
+        mx1b(0, 1, 0)
+        p1b(0, 0, 0)
+        ev_lr(0, 3)
+        mx1b(0, 0, 1)
+        p1b(0, 1, 0)
+        mx1b(0, 1, 1)
+        p1b(0, 0, 1)
+        t_wb(0, 0)
+        p1b(0, 1, 1)
+        t_wb(0, 1)
         resid(0, 0)
+        mx1b(1, 0, 0)
+        p2b(0, 0)
+        mx1b(1, 1, 0)
         resid(1, 0)
+        t_wb(1, 0)
+        p2b(0, 1)
+        mx1b(1, 0, 1)
         resid(2, 0)
+        mx1b(1, 1, 1)
+        p1b(1, 0, 0)
+        t_wb(1, 1)
+        p1b(1, 1, 0)
         resid(3, 0)
-        resid(4, 0)
-        resid(5, 0)
-        resid(6, 0)
-        resid(7, 0)
         t_q(0, 0)
-        ev_q(0, 0)
+        ld("w1", full)
         t_q(0, 1)
+        p2b(1, 0)
+        ev_q(0, 0)
         ev_q(0, 1)
+        resid(4, 0)
         t_q(0, 2)
-        ev_q(0, 2)
+        p1b(1, 0, 1)
         t_q(0, 3)
-        ev_q(0, 3)
+        ev_q(0, 2)
         t_q(1, 0)
-        ev_q(1, 0)
+        p1b(1, 1, 1)
+        ev_q(0, 3)
+        resid(5, 0)
         t_q(1, 1)
-        ev_q(1, 1)
+        p2b(1, 1)
+        ev_q(1, 0)
         t_q(1, 2)
-        ev_q(1, 2)
+        ev_q(1, 1)
+        resid(6, 0)
         t_q(1, 3)
+        gbc(1)
+        ev_q(1, 2)
         ev_q(1, 3)
         qw(0, 0)
+        rge(0, 1, 0, 512, S)
         qw(1, 0)
         qq(0, 0)
         qq(0, 1)
-        qq(1, 0)
-        qq(1, 1)
-        gb(1, 0)
-        gb(1, 1)
-        ev_gb(1)
-        gmul(1)
-        gadd(1)
-        rge(0, 1, 0, 512, S)
-        rge(1, 1, 0, 512, S)
-        resid(0, 1)
-        resid(1, 1)
-        resid(2, 1)
-        resid(3, 1)
-        resid(4, 1)
-        resid(5, 1)
-        resid(6, 1)
-        resid(7, 1)
         mx2(0, 0)
-        e1(0, 0)
+        qq(1, 0)
         mx2(0, 1)
-        e1(0, 1)
-        st(0, 0, 2)
+        rge(1, 1, 0, 512, S)
+        qq(1, 1)
         mx2(0, 2)
-        e1(0, 2)
+        bn(1)
+        resid(7, 0)
+        e1(0, 0)
         mx2(0, 3)
+        e1(0, 1)
+        bbm(1)
+        e1(0, 2)
+        st(0, 0, 2)
         e1(0, 3)
-        st(0, 2, 2)
         t_lr(1, 0)
+        ev_bb(1)
         t_lr(1, 1)
-        t_lr(1, 2)
-        t_lr(1, 3)
-        ev_lr(1, 0)
-        ev_lr(1, 1)
-        ev_lr(1, 2)
-        ev_lr(1, 3)
         qe(0, 1)
+        st(0, 2, 2)
+        t_lr(1, 2)
+        ev_lr(1, 0)
+        t_lr(1, 3)
         qe(1, 1)
+        mx1b(0, 0, 2)
+        ev_lr(1, 1)
+        resid(0, 1)
+        ev_lr(1, 2)
+        mx1b(0, 1, 2)
+        p1b(0, 0, 2)
+        ev_lr(1, 3)
+        mx1b(0, 0, 3)
+        resid(1, 1)
+        p1b(0, 1, 2)
+        mx1b(0, 1, 3)
+        p1b(0, 0, 3)
+        t_wb(0, 2)
+        resid(2, 1)
+        p1b(0, 1, 3)
+        t_wb(0, 3)
+        mx1b(1, 0, 2)
+        p2b(0, 2)
+        resid(3, 1)
+        mx1b(1, 1, 2)
+        t_wb(1, 2)
+        p2b(0, 3)
+        mx1b(1, 0, 3)
+        resid(4, 1)
+        mx1b(1, 1, 3)
+        p1b(1, 0, 2)
+        t_wb(1, 3)
+        resid(5, 1)
+        p1b(1, 1, 2)
         mx2(0, 4)
-        e1(0, 4)
+        p2b(1, 2)
         mx2(0, 5)
-        e1(0, 5)
-        st(0, 4, 2)
+        resid(6, 1)
+        p1b(1, 0, 3)
+        p1b(1, 1, 3)
+        resid(7, 1)
         mx2(0, 6)
-        e1(0, 6)
+        p2b(1, 3)
         mx2(0, 7)
-        e1(0, 7)
-        st(0, 6, 2)
-        mx1(0, 1, 0)
-        p1(0, 1, 0)
-        mx1(0, 1, 1)
-        p1(0, 1, 1)
-        mx1(0, 1, 2)
-        p1(0, 1, 2)
-        mx1(0, 1, 3)
-        p1(0, 1, 3)
-        t_w(0, 1, 0)
-        t_w(0, 1, 1)
-        mx1(1, 1, 0)
-        mx1(1, 1, 1)
-        p2(0, 1, 0)
-        p2(0, 1, 1)
-        p1(1, 1, 0)
-        p1(1, 1, 1)
-        mx1(1, 1, 2)
-        p1(1, 1, 2)
-        mx1(1, 1, 3)
-        p1(1, 1, 3)
-        t_w(1, 1, 0)
-        t_w(1, 1, 1)
-        p2(1, 1, 0)
-        p2(1, 1, 1)
         qw(0, 1)
         qw(1, 1)
+        e1(0, 4)
+        e1(0, 5)
         mx2(1, 0)
-        e1(1, 0)
+        e1(0, 6)
+        st(0, 4, 2)
         mx2(1, 1)
-        e1(1, 1)
-        st(1, 0, 2)
+        e1(0, 7)
         mx2(1, 2)
-        e1(1, 2)
+        e1(1, 0)
+        st(0, 6, 2)
         mx2(1, 3)
-        e1(1, 3)
-        st(1, 2, 2)
+        e1(1, 1)
         mx2(1, 4)
-        e1(1, 4)
+        e1(1, 2)
+        st(1, 0, 2)
         mx2(1, 5)
-        e1(1, 5)
-        st(1, 4, 2)
+        e1(1, 3)
         mx2(1, 6)
-        e1(1, 6)
-        st(1, 6, 1)
+        e1(1, 4)
+        st(1, 2, 2)
         mx2(1, 7)
+        e1(1, 5)
+        e1(1, 6)
+        st(1, 4, 2)
         e1(1, 7)
+        st(1, 6, 1)
         st(1, 7, 1)

@@ -14,6 +14,7 @@ P = 128
 T = 1024
 D = 1024
 H = 512
+Q = 256
 C = 2.0 / (T * D)
 FLOPS = 4 * T * D * D
 
@@ -33,19 +34,16 @@ def tile_tttinner_pb_kernel(tc, err, train_view, test_view, W, b, lr_w, lr_b, ou
         S = nc.scalar
         G = nc.gpsimd
         PE = nc.tensor
-        full = slice(0, D)
 
-        def hs(h):
+        def half(h):
             return slice(H * h, H * h + H)
 
-        zb = const.tile([P, P], BF16)
-        V.memset(zb[:], 0.0)
-        ones = const.tile([P, 32], BF16)
+        zr = const.tile([P, 2 * D], BF16)
+        V.memset(zr[:], 0.0)
+        ones = const.tile([P, P], BF16)
         V.memset(ones[:], 1.0)
         ident = const.tile([P, P], F32)
         make_identity(nc, ident[:])
-        ident_bf = const.tile([P, P], BF16)
-        make_identity(nc, ident_bf[:])
 
         e_codes = const.tile([P, 2, D], U32, align_bytes=64)
         e_scales = const.tile([P, 2, D], U8, align_bytes=64)
@@ -56,39 +54,22 @@ def tile_tttinner_pb_kernel(tc, err, train_view, test_view, W, b, lr_w, lr_b, ou
         q_codes = const.tile([P, 2, T], U32, align_bytes=64)
         q_scales = const.tile([P, 2, T], U8, align_bytes=64)
         lrT = const.tile([P, 4 * D], F32)
-        qb = const.tile([P, 8, D], F32)
-        bb = const.tile([P, D], F32)
-        bl = const.tile([P, 16], F32)
-        bn_col = const.tile([P, 8], F32)
         lrT_bf = lrT[:].bitcast(BF16).rearrange("p (w o e) -> p w o e", w=4, e=2)
+        qb = const.tile([P, 8, D], F32)
+        b_bc = const.tile([P, D], F32)
+        lrb = const.tile([P, D], F32)
+        gbs = const.tile([P, D], F32)
         q_view = test_view.rearrange("(p a) d -> p a d", a=8)
         out_v = out.rearrange("(p a) d -> p a d", a=8)
-        raw = {}
-        til = {}
 
-        def small2():
-            nc.sync.dma_start(out=zb[0:8, :], in_=b.rearrange("(r c) -> r c", r=8))
-            nc.sync.dma_start(out=zb[8:16, :], in_=lr_b.rearrange("(r c) -> r c", r=8))
+        def raw_tile(nm):
+            return rawp.tile([P, 4, D], BF16, tag="raw", name=nm)
 
-        def ld(nm, cols):
-            if nm not in raw:
-                raw[nm] = rawp.tile([P, 4, D], BF16, tag="raw", name=nm)
-            kind = nm[:-1]
-            n = int(nm[-1])
-            if kind == "trn":
-                src = train_view[H * n:H * n + H, cols].rearrange("(p j) w -> p j w", j=4)
-            elif kind == "err":
-                src = err[H * n:H * n + H, cols].rearrange("(p j) w -> p j w", j=4)
-            elif kind == "lr":
-                src = lr_w[hs(n), cols].rearrange("(a p) d -> p a d", p=P)
-            elif kind == "w":
-                src = W[hs(n), cols].rearrange("(a p) d -> p a d", p=P)
-            else:
-                src = q_view[:, 4 * n:4 * n + 4, cols]
-            nc.sync.dma_start(out=raw[nm][:, :, cols], in_=src)
+        def load_tokens(dst, x, gt, cols):
+            nc.sync.dma_start(out=dst[:, :, cols], in_=x[half(gt), cols].rearrange("(p j) w -> p j w", j=4))
 
-        def quantise(grouped_ap, codes, scales):
-            V.quantize_mx(out=codes.bitcast(FP8X4), scales=scales, in_=grouped_ap)
+        def load_outputs(dst, x, h, cols):
+            nc.sync.dma_start(out=dst[:, :, cols], in_=x[half(h), cols].rearrange("(a p) d -> p a d", p=P))
 
         def copy_on(eng, dst, src):
             if eng is V:
@@ -96,336 +77,166 @@ def tile_tttinner_pb_kernel(tc, err, train_view, test_view, W, b, lr_w, lr_b, ou
             else:
                 S.copy(out=dst, in_=src)
 
-        def grp_tile(key):
-            if key not in til:
-                til[key] = grp.tile([P, 4 * H], BF16, tag="grp", name="grouped", align_bytes=64)
-            return til[key]
+        def grouped_tile():
+            return grp.tile([P, 4 * H], BF16, tag="grp", name="grouped", align_bytes=64)
 
-        def t_b():
-            til["tpb"] = ps.tile([P, P], BF16, tag="tp", name="tp_b")
-            PE.transpose(til["tpb"][:], zb[:], ident_bf[:])
+        def quantise(grouped, codes, scales):
+            V.quantize_mx(out=codes.bitcast(FP8X4), scales=scales, in_=grouped)
 
-        def ev_b():
-            V.tensor_copy(out=bl[:], in_=til["tpb"][:, 0:16])
-
-        def gbc(h):
-            gcp = ps.tile([P, 4, 32], F32, tag="tp", name="gcp")
-            til[("gc", h)] = gcp
-            for k in range(4):
-                o0 = H * h + P * k
-                for r in range(8):
-                    PE.matmul(out=gcp[:, k, :], lhsT=raw["err%d" % (r // 4)][:, r % 4, o0:o0 + P], rhs=ones[:],
-                              start=(r == 0), stop=(r == 7))
-
-        def bn(h):
-            sl = slice(4 * h, 4 * h + 4)
-            V.scalar_tensor_tensor(out=bn_col[:, sl], in0=til[("gc", h)][:, :, 0], scalar=-C,
-                                   in1=bl[:, 8 + 4 * h:12 + 4 * h], op0=ALU.mult, op1=ALU.mult)
-            V.tensor_tensor(out=bn_col[:, sl], in0=bn_col[:, sl], in1=bl[:, sl], op=ALU.add)
-
-        def bbm(h):
-            bbp = ps.tile([P, H], F32, tag="tp", name="bbp")
-            til[("bbp", h)] = bbp
-            for k in range(4):
-                PE.matmul(out=bbp[:, P * k:P * k + P],
-                          lhsT=bn_col[:, 4 * h + k:4 * h + k + 1].to_broadcast([P, P]), rhs=ident[:],
-                          start=True, stop=True)
-
-        def ev_bb(h):
-            S.copy(out=bb[:, hs(h)], in_=til[("bbp", h)][:])
-
-        def rge(gt, h, c0, c1, eng):
-            ge = grp_tile(("e", gt, h))
-            copy_on(eng, ge[:, 4 * c0:4 * c1].rearrange("p (c i t) -> p c t i", i=4, t=4),
-                    raw["err%d" % gt][:, :, H * h + c0:H * h + c1].rearrange("p t (c i) -> p c t i", i=4))
-
-        def qe(gt, h):
-            quantise(til[("e", gt, h)][:], e_codes[:, gt, hs(h)], e_scales[:, gt, hs(h)])
-
-        def rgt(gt, g, u, eng):
-            gr = grp_tile(("t", gt, g))
-            copy_on(eng, gr[:, 1024 * u:1024 * (u + 1)].rearrange("p (e q j) -> p q e j", e=2, j=4),
-                    raw["trn%d" % gt][:, :, H * g + 256 * u:H * g + 256 * (u + 1)].rearrange(
-                        "p j (q e) -> p q e j", e=2))
-
-        def qt(gt, g):
-            quantise(til[("t", gt, g)][:], t_codes[:, gt, hs(g)], t_scales[:, gt, hs(g)])
-
-        def t_lr(h, wb):
-            tp = ps.tile([P, H], F32, tag="tp", name="tp_lr")
-            til[("lrp", h, wb)] = tp
-            for ab in range(4):
-                PE.transpose(tp[:, P * ab:P * ab + P],
-                             raw["lr%d" % h][:, ab, :].bitcast(F32)[:, P * wb:P * wb + P], ident[:])
-
-        def ev_lr(h, wb):
-            S.copy(out=lrT[:, D * wb + H * h:D * wb + H * h + H], in_=til[("lrp", h, wb)][:])
-
-        def mx1b(g, u, oq):
-            acc = ps.tile([P, H], F32, tag="acc", name="acc1")
-            til[("a1", g, u, oq)] = acc
-            oc = slice(256 * oq, 256 * oq + 256)
-            for e in range(2):
-                w0 = H * g + 256 * u + P * e
-                for gt in range(2):
-                    PE.matmul_mx(out=acc[:, 256 * e:256 * e + 256],
-                                 lhsT=t_codes[:, gt, w0:w0 + P].bitcast(FP8X4),
-                                 lhsT_scale=t_scales[:, gt, w0:w0 + P],
-                                 rhs=e_codes[:, gt, oc].bitcast(FP8X4), rhs_scale=e_scales[:, gt, oc],
-                                 start=(gt == 0), stop=(gt == 1))
-
-        def p1b(g, u, oq):
-            if ("tmp", g, oq) not in til:
-                til[("tmp", g, oq)] = tmpp.tile([P, 2, H], F32, tag="tmp", name="tmp")
-            V.scalar_tensor_tensor(out=til[("tmp", g, oq)][:, u, :].rearrange("p (o e) -> p o e", e=2),
-                                   in0=til[("a1", g, u, oq)][:].rearrange("p (e o) -> p o e", e=2), scalar=-C,
-                                   in1=lrT_bf[:, 2 * g + u, 256 * oq:256 * oq + 256, :],
-                                   op0=ALU.mult, op1=ALU.mult)
-
-        def t_wb(g, oq):
-            tp = ps.tile([P, H], F32, tag="tp", name="tp_w")
-            til[("wp", g, oq)] = tp
+        def regroup_train(gt, g, eng):
+            gr = grouped_tile()
             for u in range(2):
-                for k in range(2):
-                    wb = 2 * g + u
-                    PE.transpose(tp[:, 256 * u + P * k:256 * u + P * k + P],
-                                 raw["w%d" % (oq // 2)][:, 2 * (oq % 2) + k, :].bitcast(F32)[:, P * wb:P * wb + P],
-                                 ident[:])
+                c0 = H * g + Q * u
+                copy_on(eng, gr[:, 4 * Q * u:4 * Q * (u + 1)].rearrange("p (e q j) -> p q e j", e=2, j=4),
+                        trn_raw[gt][:, :, c0:c0 + Q].rearrange("p j (q e) -> p q e j", e=2))
+            return gr
 
-        def p2b(g, oq):
-            gw = grp_tile(("w", g, oq // 2))
-            c0 = 1024 * (oq % 2)
-            V.tensor_tensor(out=gw[:, c0:c0 + 1024].rearrange("p (o u e) -> p o u e", u=2, e=2),
-                            in0=til[("tmp", g, oq)][:].rearrange("p u (o e) -> p o u e", e=2),
-                            in1=til[("wp", g, oq)][:].bitcast(BF16).rearrange("p (u o e) -> p o u e", u=2, e=2),
-                            op=ALU.add)
+        def regroup_err(gt, h, shares):
+            ge = grouped_tile()
+            for eng, c0, c1 in shares:
+                copy_on(eng, ge[:, 4 * c0:4 * c1].rearrange("p (c i t) -> p c t i", i=4, t=4),
+                        err_raw[gt][:, :, H * h + c0:H * h + c1].rearrange("p t (c i) -> p c t i", i=4))
+            return ge
 
-        def qw(g, h):
-            quantise(til[("w", g, h)][:], w_codes[:, g, hs(h)], w_scales[:, g, hs(h)])
+        def column_sums(acc, h, gt):
+            for j in range(4):
+                PE.matmul(out=acc[:], lhsT=ones[:], rhs=err_raw[gt][:, j, half(h)],
+                          start=(gt == 0 and j == 0), stop=(gt == 1 and j == 3))
 
-        def t_q(c, a4):
-            tp = ps.tile([P, 4, P], F32, tag="tp", name="tp_q")
-            til[("qp", c, a4)] = tp
+        def transpose_rates(h):
             for wb in range(4):
-                PE.transpose(tp[:, wb, :], raw["q%d" % c][:, a4, :].bitcast(F32)[:, P * wb:P * wb + P], ident[:])
+                tp = ps.tile([P, H], F32, tag="tp", name="tp_lr")
+                for ab in range(4):
+                    PE.transpose(tp[:, P * ab:P * ab + P],
+                                 lr_raw[h][:, ab, :].bitcast(F32)[:, P * wb:P * wb + P], ident[:])
+                S.copy(out=lrT[:, D * wb + H * h:D * wb + H * h + H], in_=tp[:])
 
-        def ev_q(c, a4):
-            if ("gq", c) not in til:
-                til[("gq", c)] = gqp.tile([P, 2 * 4 * H], BF16, tag="gq", name="gq", align_bytes=64)
-            gq_w = til[("gq", c)][:].bitcast(F32).rearrange("p (g t u) -> p g t u", g=2, u=2)
-            S.copy(out=gq_w[:, :, P * a4:P * a4 + P, :],
-                   in_=til[("qp", c, a4)][:].rearrange("p (g u) t -> p g t u", g=2))
+        def bias_and_residual(h, sums):
+            spread = []
+            for k in (h, 2 + h):
+                pb = ps.tile([P, H], F32, tag="tp", name="pb")
+                spread.append(pb)
+                PE.matmul(out=pb[:], lhsT=ones[:], rhs=zr[:, H * k:H * k + H], start=True, stop=True)
+            S.copy(out=b_bc[:, half(h)], in_=spread[0][:])
+            S.copy(out=lrb[:, half(h)], in_=spread[1][:])
+            S.mul(out=gbs[:, half(h)], in_=sums[:], mul=-C)
+            G.tensor_tensor(out=gbs[:, half(h)], in0=gbs[:, half(h)], in1=lrb[:, half(h)], op=ALU.mult)
+            G.tensor_tensor(out=b_bc[:, half(h)], in0=gbs[:, half(h)], in1=b_bc[:, half(h)], op=ALU.add)
+            for a in range(8):
+                G.tensor_tensor(out=qb[:, a, half(h)], in0=q_raw[a // 4][:, a % 4, half(h)], in1=b_bc[:, half(h)],
+                                op=ALU.add)
 
-        def qq(c, g):
-            quantise(til[("gq", c)][:, 4 * H * g:4 * H * (g + 1)], q_codes[:, g, hs(c)], q_scales[:, g, hs(c)])
-
-        def resid(a, h):
-            G.tensor_tensor(out=qb[:, a, hs(h)], in0=raw["q%d" % (a // 4)][:, a % 4, hs(h)], in1=bb[:, hs(h)],
-                            op=ALU.add)
-
-        def mx2(h, a):
-            acc = ps.tile([P, H], F32, tag="acc", name="acc2")
-            til[("a2", h, a)] = acc
+        def new_weights(h):
             for g in range(2):
-                PE.matmul_mx(out=acc[:],
-                             lhsT=q_codes[:, g, P * a:P * a + P].bitcast(FP8X4),
-                             lhsT_scale=q_scales[:, g, P * a:P * a + P],
-                             rhs=w_codes[:, g, hs(h)].bitcast(FP8X4), rhs_scale=w_scales[:, g, hs(h)],
-                             start=(g == 0), stop=(g == 1))
+                gw = grouped_tile()
+                for oq in (2 * h, 2 * h + 1):
+                    oc = slice(Q * oq, Q * oq + Q)
+                    accs = []
+                    for u in range(2):
+                        acc = ps.tile([P, H], F32, tag="acc", name="acc1")
+                        accs.append(acc)
+                        for e in range(2):
+                            w0 = H * g + Q * u + P * e
+                            for gt in range(2):
+                                PE.matmul_mx(out=acc[:, Q * e:Q * e + Q],
+                                             lhsT=t_codes[:, gt, w0:w0 + P].bitcast(FP8X4),
+                                             lhsT_scale=t_scales[:, gt, w0:w0 + P],
+                                             rhs=e_codes[:, gt, oc].bitcast(FP8X4), rhs_scale=e_scales[:, gt, oc],
+                                             start=(gt == 0), stop=(gt == 1))
+                    wp = ps.tile([P, H], F32, tag="tp", name="tp_w")
+                    for u in range(2):
+                        for k in range(2):
+                            wb = 2 * g + u
+                            PE.transpose(wp[:, Q * u + P * k:Q * u + P * k + P],
+                                         w_raw[h][:, 2 * (oq % 2) + k, :].bitcast(F32)[:, P * wb:P * wb + P],
+                                         ident[:])
+                    tmp = tmpp.tile([P, 2, H], F32, tag="tmp", name="tmp")
+                    for u in range(2):
+                        V.scalar_tensor_tensor(out=tmp[:, u, :].rearrange("p (o e) -> p o e", e=2),
+                                               in0=accs[u][:].rearrange("p (e o) -> p o e", e=2), scalar=-C,
+                                               in1=lrT_bf[:, 2 * g + u, oc, :], op0=ALU.mult, op1=ALU.mult)
+                    c0 = 4 * Q * (oq % 2)
+                    V.tensor_tensor(out=gw[:, c0:c0 + 4 * Q].rearrange("p (o u e) -> p o u e", u=2, e=2),
+                                    in0=tmp[:].rearrange("p u (o e) -> p o u e", e=2),
+                                    in1=wp[:].bitcast(BF16).rearrange("p (u o e) -> p o u e", u=2, e=2),
+                                    op=ALU.add)
+                quantise(gw[:], w_codes[:, g, half(h)], w_scales[:, g, half(h)])
 
-        def e1(h, a):
-            V.tensor_tensor(out=qb[:, a, hs(h)], in0=til[("a2", h, a)][:], in1=qb[:, a, hs(h)], op=ALU.add)
+        def transpose_query(c):
+            gq = gqp.tile([P, 2 * 4 * H], BF16, tag="gq", name="gq", align_bytes=64)
+            gq_w = gq[:].bitcast(F32).rearrange("p (g t u) -> p g t u", g=2, u=2)
+            for a4 in range(4):
+                tp = ps.tile([P, 4, P], F32, tag="tp", name="tp_q")
+                for wb in range(4):
+                    PE.transpose(tp[:, wb, :], q_raw[c][:, a4, :].bitcast(F32)[:, P * wb:P * wb + P], ident[:])
+                S.copy(out=gq_w[:, :, P * a4:P * a4 + P, :], in_=tp[:].rearrange("p (g u) t -> p g t u", g=2))
+            return gq
 
-        def st(h, a, n):
-            nc.sync.dma_start(out=out_v[:, a:a + n, hs(h)], in_=qb[:, a:a + n, hs(h)])
+        def query(h):
+            for a in range(8):
+                acc = ps.tile([P, H], F32, tag="acc", name="acc2")
+                for g in range(2):
+                    PE.matmul_mx(out=acc[:],
+                                 lhsT=q_codes[:, g, P * a:P * a + P].bitcast(FP8X4),
+                                 lhsT_scale=q_scales[:, g, P * a:P * a + P],
+                                 rhs=w_codes[:, g, half(h)].bitcast(FP8X4), rhs_scale=w_scales[:, g, half(h)],
+                                 start=(g == 0), stop=(g == 1))
+                V.tensor_tensor(out=qb[:, a, half(h)], in0=acc[:], in1=qb[:, a, half(h)], op=ALU.add)
+                if h == 1 and a >= 6:
+                    nc.sync.dma_start(out=out_v[:, a, half(h)], in_=qb[:, a, half(h)])
+                elif a % 2 == 1:
+                    nc.sync.dma_start(out=out_v[:, a - 1:a + 1, half(h)], in_=qb[:, a - 1:a + 1, half(h)])
 
-        ld("trn0", full)
-        small2()
-        ld("err0", hs(0))
-        ld("trn1", full)
-        ld("err1", hs(0))
-        ld("lr0", hs(0))
-        ld("lr0", hs(1))
-        ld("w0", full)
-        rgt(0, 0, 0, V)
-        rgt(0, 1, 0, S)
-        t_b()
-        rgt(0, 0, 1, V)
-        rgt(0, 1, 1, S)
-        gbc(0)
-        qt(0, 0)
-        rge(0, 0, 0, 512, V)
-        ld("q0", full)
-        qt(0, 1)
-        rgt(1, 1, 0, S)
-        qe(0, 0)
-        rgt(1, 0, 0, V)
-        rgt(1, 1, 1, S)
-        rgt(1, 0, 1, V)
-        ev_b()
-        rge(1, 0, 256, 512, S)
-        ld("q1", full)
-        qt(1, 1)
-        ld("err0", hs(1))
-        t_lr(0, 0)
-        ld("err1", hs(1))
-        t_lr(0, 1)
-        bn(0)
-        rge(1, 0, 0, 256, V)
-        ev_lr(0, 0)
-        t_lr(0, 2)
-        qt(1, 0)
-        bbm(0)
-        ev_lr(0, 1)
-        qe(1, 0)
-        t_lr(0, 3)
-        ev_bb(0)
-        mx1b(0, 0, 0)
-        ld("lr1", full)
-        ev_lr(0, 2)
-        mx1b(0, 1, 0)
-        p1b(0, 0, 0)
-        ev_lr(0, 3)
-        mx1b(0, 0, 1)
-        p1b(0, 1, 0)
-        mx1b(0, 1, 1)
-        p1b(0, 0, 1)
-        t_wb(0, 0)
-        p1b(0, 1, 1)
-        t_wb(0, 1)
-        resid(0, 0)
-        mx1b(1, 0, 0)
-        p2b(0, 0)
-        mx1b(1, 1, 0)
-        resid(1, 0)
-        t_wb(1, 0)
-        p2b(0, 1)
-        mx1b(1, 0, 1)
-        resid(2, 0)
-        mx1b(1, 1, 1)
-        p1b(1, 0, 0)
-        t_wb(1, 1)
-        p1b(1, 1, 0)
-        resid(3, 0)
-        t_q(0, 0)
-        ld("w1", full)
-        t_q(0, 1)
-        p2b(1, 0)
-        ev_q(0, 0)
-        ev_q(0, 1)
-        resid(4, 0)
-        t_q(0, 2)
-        p1b(1, 0, 1)
-        t_q(0, 3)
-        ev_q(0, 2)
-        t_q(1, 0)
-        p1b(1, 1, 1)
-        ev_q(0, 3)
-        resid(5, 0)
-        t_q(1, 1)
-        p2b(1, 1)
-        ev_q(1, 0)
-        t_q(1, 2)
-        ev_q(1, 1)
-        resid(6, 0)
-        t_q(1, 3)
-        gbc(1)
-        ev_q(1, 2)
-        ev_q(1, 3)
-        qw(0, 0)
-        rge(0, 1, 0, 512, S)
-        qw(1, 0)
-        qq(0, 0)
-        qq(0, 1)
-        mx2(0, 0)
-        qq(1, 0)
-        mx2(0, 1)
-        rge(1, 1, 0, 512, S)
-        qq(1, 1)
-        mx2(0, 2)
-        bn(1)
-        resid(7, 0)
-        e1(0, 0)
-        mx2(0, 3)
-        e1(0, 1)
-        bbm(1)
-        e1(0, 2)
-        st(0, 0, 2)
-        e1(0, 3)
-        t_lr(1, 0)
-        ev_bb(1)
-        t_lr(1, 1)
-        qe(0, 1)
-        st(0, 2, 2)
-        t_lr(1, 2)
-        ev_lr(1, 0)
-        t_lr(1, 3)
-        qe(1, 1)
-        mx1b(0, 0, 2)
-        ev_lr(1, 1)
-        resid(0, 1)
-        ev_lr(1, 2)
-        mx1b(0, 1, 2)
-        p1b(0, 0, 2)
-        ev_lr(1, 3)
-        mx1b(0, 0, 3)
-        resid(1, 1)
-        p1b(0, 1, 2)
-        mx1b(0, 1, 3)
-        p1b(0, 0, 3)
-        t_wb(0, 2)
-        resid(2, 1)
-        p1b(0, 1, 3)
-        t_wb(0, 3)
-        mx1b(1, 0, 2)
-        p2b(0, 2)
-        resid(3, 1)
-        mx1b(1, 1, 2)
-        t_wb(1, 2)
-        p2b(0, 3)
-        mx1b(1, 0, 3)
-        resid(4, 1)
-        mx1b(1, 1, 3)
-        p1b(1, 0, 2)
-        t_wb(1, 3)
-        resid(5, 1)
-        p1b(1, 1, 2)
-        mx2(0, 4)
-        p2b(1, 2)
-        mx2(0, 5)
-        resid(6, 1)
-        p1b(1, 0, 3)
-        p1b(1, 1, 3)
-        resid(7, 1)
-        mx2(0, 6)
-        p2b(1, 3)
-        mx2(0, 7)
-        qw(0, 1)
-        qw(1, 1)
-        e1(0, 4)
-        e1(0, 5)
-        mx2(1, 0)
-        e1(0, 6)
-        st(0, 4, 2)
-        mx2(1, 1)
-        e1(0, 7)
-        mx2(1, 2)
-        e1(1, 0)
-        st(0, 6, 2)
-        mx2(1, 3)
-        e1(1, 1)
-        mx2(1, 4)
-        e1(1, 2)
-        st(1, 0, 2)
-        mx2(1, 5)
-        e1(1, 3)
-        mx2(1, 6)
-        e1(1, 4)
-        st(1, 2, 2)
-        mx2(1, 7)
-        e1(1, 5)
-        e1(1, 6)
-        st(1, 4, 2)
-        e1(1, 7)
-        st(1, 6, 1)
-        st(1, 7, 1)
+        trn_raw = [raw_tile("trn_raw0"), raw_tile("trn_raw1")]
+        err_raw = [raw_tile("err_raw0"), raw_tile("err_raw1")]
+        lr_raw = [raw_tile("lr_raw0")]
+        w_raw = [raw_tile("w_raw0")]
+        load_tokens(trn_raw[0], train_view, 0, slice(0, D))
+        load_tokens(err_raw[0], err, 0, half(0))
+        nc.sync.dma_start(out=zr[0:1, 0:D], in_=b.rearrange("(o d) -> o d", o=1))
+        nc.sync.dma_start(out=zr[0:1, D:2 * D], in_=lr_b.rearrange("(o d) -> o d", o=1))
+        load_tokens(trn_raw[1], train_view, 1, slice(0, D))
+        load_tokens(err_raw[1], err, 1, half(0))
+        load_outputs(lr_raw[0], lr_w, 0, half(0))
+        load_outputs(lr_raw[0], lr_w, 0, half(1))
+        load_outputs(w_raw[0], W, 0, slice(0, D))
+
+        sums = [ps.tile([P, H], F32, tag="tp", name="sums0")]
+        for gt in range(2):
+            gr0 = regroup_train(gt, 0, V)
+            gr1 = regroup_train(gt, 1, S)
+            ge = regroup_err(gt, 0, ((V, 0, Q), (S, Q, H)))
+            quantise(gr0[:], t_codes[:, gt, half(0)], t_scales[:, gt, half(0)])
+            quantise(gr1[:], t_codes[:, gt, half(1)], t_scales[:, gt, half(1)])
+            quantise(ge[:], e_codes[:, gt, half(0)], e_scales[:, gt, half(0)])
+            column_sums(sums[0], 0, gt)
+        for gt in range(2):
+            load_tokens(err_raw[gt], err, gt, half(1))
+        q_raw = []
+        for c in range(2):
+            q_raw.append(raw_tile("q_raw%d" % c))
+            nc.sync.dma_start(out=q_raw[c][:], in_=q_view[:, 4 * c:4 * c + 4, :])
+
+        transpose_rates(0)
+        bias_and_residual(0, sums[0])
+        lr_raw.append(raw_tile("lr_raw1"))
+        load_outputs(lr_raw[1], lr_w, 1, slice(0, D))
+        new_weights(0)
+        w_raw.append(raw_tile("w_raw1"))
+        load_outputs(w_raw[1], W, 1, slice(0, D))
+
+        sums.append(ps.tile([P, H], F32, tag="tp", name="sums1"))
+        for gt in range(2):
+            ge = regroup_err(gt, 1, ((S, 0, H),))
+            quantise(ge[:], e_codes[:, gt, half(1)], e_scales[:, gt, half(1)])
+            column_sums(sums[1], 1, gt)
+        transpose_rates(1)
+        bias_and_residual(1, sums[1])
+        new_weights(1)
+
+        for c in range(2):
+            gq = transpose_query(c)
+            for g in range(2):
+                quantise(gq[:, 4 * H * g:4 * H * (g + 1)], q_codes[:, g, half(c)], q_scales[:, g, half(c)])
+        for h in range(2):
+            query(h)

@@ -126,41 +126,56 @@ def tile_tttinner_pb_kernel(tc, err, train_view, test_view, W, b, lr_w, lr_b, ou
                 G.tensor_tensor(out=qb[:, a, half(h)], in0=q_raw[a // 4][:, a % 4, half(h)], in1=b_bc[:, half(h)],
                                 op=ALU.add)
 
+        def multiply(g, oq):
+            oc = slice(Q * oq, Q * oq + Q)
+            accs = []
+            for u in range(2):
+                acc = ps.tile([P, H], F32, tag="acc", name="acc1")
+                accs.append(acc)
+                for e in range(2):
+                    w0 = H * g + Q * u + P * e
+                    for gt in range(2):
+                        PE.matmul_mx(out=acc[:, Q * e:Q * e + Q],
+                                     lhsT=t_codes[:, gt, w0:w0 + P].bitcast(FP8X4),
+                                     lhsT_scale=t_scales[:, gt, w0:w0 + P],
+                                     rhs=e_codes[:, gt, oc].bitcast(FP8X4), rhs_scale=e_scales[:, gt, oc],
+                                     start=(gt == 0), stop=(gt == 1))
+            wp = ps.tile([P, H], F32, tag="tp", name="tp_w")
+            for u in range(2):
+                for k in range(2):
+                    wb = 2 * g + u
+                    PE.transpose(wp[:, Q * u + P * k:Q * u + P * k + P],
+                                 w_raw[oq // 2][:, 2 * (oq % 2) + k, :].bitcast(F32)[:, P * wb:P * wb + P],
+                                 ident[:])
+            tmp = tmpp.tile([P, 2, H], F32, tag="tmp", name="tmp")
+            for u in range(2):
+                V.scalar_tensor_tensor(out=tmp[:, u, :].rearrange("p (o e) -> p o e", e=2),
+                                       in0=accs[u][:].rearrange("p (e o) -> p o e", e=2), scalar=-C,
+                                       in1=lrT_bf[:, 2 * g + u, oc, :], op0=ALU.mult, op1=ALU.mult)
+            return tmp, wp
+
+        def add(gw, oq, tmp, wp):
+            c0 = 4 * Q * (oq % 2)
+            V.tensor_tensor(out=gw[:, c0:c0 + 4 * Q].rearrange("p (o u e) -> p o u e", u=2, e=2),
+                            in0=tmp[:].rearrange("p u (o e) -> p o u e", e=2),
+                            in1=wp[:].bitcast(BF16).rearrange("p (u o e) -> p o u e", u=2, e=2),
+                            op=ALU.add)
+
         def new_weights(h):
+            grouped = [grouped_tile(), grouped_tile()]
+            waiting = None
             for g in range(2):
-                gw = grouped_tile()
                 for oq in (2 * h, 2 * h + 1):
-                    oc = slice(Q * oq, Q * oq + Q)
-                    accs = []
-                    for u in range(2):
-                        acc = ps.tile([P, H], F32, tag="acc", name="acc1")
-                        accs.append(acc)
-                        for e in range(2):
-                            w0 = H * g + Q * u + P * e
-                            for gt in range(2):
-                                PE.matmul_mx(out=acc[:, Q * e:Q * e + Q],
-                                             lhsT=t_codes[:, gt, w0:w0 + P].bitcast(FP8X4),
-                                             lhsT_scale=t_scales[:, gt, w0:w0 + P],
-                                             rhs=e_codes[:, gt, oc].bitcast(FP8X4), rhs_scale=e_scales[:, gt, oc],
-                                             start=(gt == 0), stop=(gt == 1))
-                    wp = ps.tile([P, H], F32, tag="tp", name="tp_w")
-                    for u in range(2):
-                        for k in range(2):
-                            wb = 2 * g + u
-                            PE.transpose(wp[:, Q * u + P * k:Q * u + P * k + P],
-                                         w_raw[h][:, 2 * (oq % 2) + k, :].bitcast(F32)[:, P * wb:P * wb + P],
-                                         ident[:])
-                    tmp = tmpp.tile([P, 2, H], F32, tag="tmp", name="tmp")
-                    for u in range(2):
-                        V.scalar_tensor_tensor(out=tmp[:, u, :].rearrange("p (o e) -> p o e", e=2),
-                                               in0=accs[u][:].rearrange("p (e o) -> p o e", e=2), scalar=-C,
-                                               in1=lrT_bf[:, 2 * g + u, oc, :], op0=ALU.mult, op1=ALU.mult)
-                    c0 = 4 * Q * (oq % 2)
-                    V.tensor_tensor(out=gw[:, c0:c0 + 4 * Q].rearrange("p (o u e) -> p o u e", u=2, e=2),
-                                    in0=tmp[:].rearrange("p u (o e) -> p o u e", e=2),
-                                    in1=wp[:].bitcast(BF16).rearrange("p (u o e) -> p o u e", u=2, e=2),
-                                    op=ALU.add)
-                quantise(gw[:], w_codes[:, g, half(h)], w_scales[:, g, half(h)])
+                    product = multiply(g, oq)
+                    if waiting is not None:
+                        add(*waiting)
+                    waiting = (grouped[g], oq) + product
+            add(*waiting)
+            return grouped
+
+        def quantise_weights(h, grouped):
+            for g in range(2):
+                quantise(grouped[g][:], w_codes[:, g, half(h)], w_scales[:, g, half(h)])
 
         def transpose_query(c):
             gq = gqp.tile([P, 2 * 4 * H], BF16, tag="gq", name="gq", align_bytes=64)
@@ -221,7 +236,7 @@ def tile_tttinner_pb_kernel(tc, err, train_view, test_view, W, b, lr_w, lr_b, ou
         bias_and_residual(0, sums[0])
         lr_raw.append(raw_tile("lr_raw1"))
         load_outputs(lr_raw[1], lr_w, 1, slice(0, D))
-        new_weights(0)
+        gw0 = new_weights(0)
         w_raw.append(raw_tile("w_raw1"))
         load_outputs(w_raw[1], W, 1, slice(0, D))
 
@@ -230,13 +245,15 @@ def tile_tttinner_pb_kernel(tc, err, train_view, test_view, W, b, lr_w, lr_b, ou
             ge = regroup_err(gt, 1, ((S, 0, H),))
             quantise(ge[:], e_codes[:, gt, half(1)], e_scales[:, gt, half(1)])
             column_sums(sums[1], 1, gt)
+        quantise_weights(0, gw0)
         transpose_rates(1)
         bias_and_residual(1, sums[1])
-        new_weights(1)
+        gw1 = new_weights(1)
 
+        gq = [transpose_query(c) for c in range(2)]
+        quantise_weights(1, gw1)
         for c in range(2):
-            gq = transpose_query(c)
             for g in range(2):
-                quantise(gq[:, 4 * H * g:4 * H * (g + 1)], q_codes[:, g, half(c)], q_scales[:, g, half(c)])
+                quantise(gq[c][:, 4 * H * g:4 * H * (g + 1)], q_codes[:, g, half(c)], q_scales[:, g, half(c)])
         for h in range(2):
             query(h)

@@ -27,7 +27,7 @@ def tile_tttinner_pb_kernel(tc, err, train_view, test_view, W, b, lr_w, lr_b, ou
         grp = ctx.enter_context(tc.tile_pool(name="grp", bufs=6))
         gqp = ctx.enter_context(tc.tile_pool(name="gqp", bufs=2))
         tmpp = ctx.enter_context(tc.tile_pool(name="tmpp", bufs=4))
-        ps = ctx.enter_context(tc.psum_pool(name="ps", bufs=4))
+        ps = ctx.enter_context(tc.psum_pool(name="ps", bufs=8))
         ctx.enter_context(tc.manual_schedule())
 
         V = nc.vector
@@ -105,7 +105,7 @@ def tile_tttinner_pb_kernel(tc, err, train_view, test_view, W, b, lr_w, lr_b, ou
 
         def transpose_rates(h):
             for wb in range(4):
-                tp = ps.tile([P, H], F32, tag="tp", name="tp_lr")
+                tp = ps.tile([P, H], F32, tag="bank", name="tp_lr")
                 for ab in range(4):
                     PE.transpose(tp[:, P * ab:P * ab + P],
                                  lr_raw[h][:, ab, :].bitcast(F32)[:, P * wb:P * wb + P], ident[:])
@@ -114,7 +114,7 @@ def tile_tttinner_pb_kernel(tc, err, train_view, test_view, W, b, lr_w, lr_b, ou
         def bias_and_residual(h, sums):
             spread = []
             for k in (h, 2 + h):
-                pb = ps.tile([P, H], F32, tag="tp", name="pb")
+                pb = ps.tile([P, H], F32, tag="bank", name="pb")
                 spread.append(pb)
                 PE.matmul(out=pb[:], lhsT=ones[:], rhs=zr[:, H * k:H * k + H], start=True, stop=True)
             S.copy(out=b_bc[:, half(h)], in_=spread[0][:])
@@ -130,7 +130,7 @@ def tile_tttinner_pb_kernel(tc, err, train_view, test_view, W, b, lr_w, lr_b, ou
             oc = slice(Q * oq, Q * oq + Q)
             accs = []
             for u in range(2):
-                acc = ps.tile([P, H], F32, tag="acc", name="acc1")
+                acc = ps.tile([P, H], F32, tag="bank", name="acc1")
                 accs.append(acc)
                 for e in range(2):
                     w0 = H * g + Q * u + P * e
@@ -140,7 +140,7 @@ def tile_tttinner_pb_kernel(tc, err, train_view, test_view, W, b, lr_w, lr_b, ou
                                      lhsT_scale=t_scales[:, gt, w0:w0 + P],
                                      rhs=e_codes[:, gt, oc].bitcast(FP8X4), rhs_scale=e_scales[:, gt, oc],
                                      start=(gt == 0), stop=(gt == 1))
-            wp = ps.tile([P, H], F32, tag="tp", name="tp_w")
+            wp = ps.tile([P, H], F32, tag="bank", name="tp_w")
             for u in range(2):
                 for k in range(2):
                     wb = 2 * g + u
@@ -181,7 +181,7 @@ def tile_tttinner_pb_kernel(tc, err, train_view, test_view, W, b, lr_w, lr_b, ou
             gq = gqp.tile([P, 2 * 4 * H], BF16, tag="gq", name="gq", align_bytes=64)
             gq_w = gq[:].bitcast(F32).rearrange("p (g t u) -> p g t u", g=2, u=2)
             for a4 in range(4):
-                tp = ps.tile([P, 4, P], F32, tag="tp", name="tp_q")
+                tp = ps.tile([P, 4, P], F32, tag="bank", name="tp_q")
                 for wb in range(4):
                     PE.transpose(tp[:, wb, :], q_raw[c][:, a4, :].bitcast(F32)[:, P * wb:P * wb + P], ident[:])
                 S.copy(out=gq_w[:, :, P * a4:P * a4 + P, :], in_=tp[:].rearrange("p (g u) t -> p g t u", g=2))
@@ -189,7 +189,7 @@ def tile_tttinner_pb_kernel(tc, err, train_view, test_view, W, b, lr_w, lr_b, ou
 
         def query(h):
             for a in range(8):
-                acc = ps.tile([P, H], F32, tag="acc", name="acc2")
+                acc = ps.tile([P, H], F32, tag="bank", name="acc2")
                 for g in range(2):
                     PE.matmul_mx(out=acc[:],
                                  lhsT=q_codes[:, g, P * a:P * a + P].bitcast(FP8X4),
@@ -216,7 +216,7 @@ def tile_tttinner_pb_kernel(tc, err, train_view, test_view, W, b, lr_w, lr_b, ou
         load_outputs(lr_raw[0], lr_w, 0, half(1))
         load_outputs(w_raw[0], W, 0, slice(0, D))
 
-        sums = [ps.tile([P, H], F32, tag="tp", name="sums0")]
+        sums = [ps.tile([P, H], F32, tag="bank", name="sums0")]
         for gt in range(2):
             gr0 = regroup_train(gt, 0, V)
             gr1 = regroup_train(gt, 1, S)
@@ -240,7 +240,7 @@ def tile_tttinner_pb_kernel(tc, err, train_view, test_view, W, b, lr_w, lr_b, ou
         w_raw.append(raw_tile("w_raw1"))
         load_outputs(w_raw[1], W, 1, slice(0, D))
 
-        sums.append(ps.tile([P, H], F32, tag="tp", name="sums1"))
+        sums.append(ps.tile([P, H], F32, tag="bank", name="sums1"))
         for gt in range(2):
             ge = regroup_err(gt, 1, ((S, 0, H),))
             quantise(ge[:], e_codes[:, gt, half(1)], e_scales[:, gt, half(1)])

@@ -44,6 +44,8 @@ def tile_tttinner_pb_kernel(tc, err, train_view, test_view, W, b, lr_w, lr_b, ou
         V.memset(ones[:], 1.0)
         ident = const.tile([P, P], F32)
         make_identity(nc, ident[:])
+        warm = const.tile([P, 1], F32)
+        G.tensor_tensor(out=warm[:], in0=ident[:, 0:1], in1=ident[:, 0:1], op=ALU.add)
 
         e_codes = const.tile([P, 2, D], U32, align_bytes=64)
         e_scales = const.tile([P, 2, D], U8, align_bytes=64)

@@ -113,7 +113,10 @@ def tile_tttinner_pb_kernel(tc, err, train_view, test_view, W, b, lr_w, lr_b, ou
                                  lr_raw[h][:, ab, :].bitcast(F32)[:, P * wb:P * wb + P], ident[:])
                 S.copy(out=lrT[:, D * wb + H * h:D * wb + H * h + H], in_=tp[:])
 
-        def bias_and_residual(h, sums):
+        def scale_sums(h, sums):
+            S.mul(out=gbs[:, half(h)], in_=sums[:], mul=-C)
+
+        def bias_and_residual(h):
             spread = []
             for k in (h, 2 + h):
                 pb = ps.tile([P, H], F32, tag="bank", name="pb")
@@ -121,7 +124,6 @@ def tile_tttinner_pb_kernel(tc, err, train_view, test_view, W, b, lr_w, lr_b, ou
                 PE.matmul(out=pb[:], lhsT=ones[:], rhs=zr[:, H * k:H * k + H], start=True, stop=True)
             S.copy(out=b_bc[:, half(h)], in_=spread[0][:])
             S.copy(out=lrb[:, half(h)], in_=spread[1][:])
-            S.mul(out=gbs[:, half(h)], in_=sums[:], mul=-C)
             G.tensor_tensor(out=gbs[:, half(h)], in0=gbs[:, half(h)], in1=lrb[:, half(h)], op=ALU.mult)
             G.tensor_tensor(out=b_bc[:, half(h)], in0=gbs[:, half(h)], in1=b_bc[:, half(h)], op=ALU.add)
             for a in range(8):
@@ -234,8 +236,9 @@ def tile_tttinner_pb_kernel(tc, err, train_view, test_view, W, b, lr_w, lr_b, ou
             q_raw.append(raw_tile("q_raw%d" % c))
             nc.sync.dma_start(out=q_raw[c][:], in_=q_view[:, 4 * c:4 * c + 4, :])
 
+        scale_sums(0, sums[0])
         transpose_rates(0)
-        bias_and_residual(0, sums[0])
+        bias_and_residual(0)
         lr_raw.append(raw_tile("lr_raw1"))
         load_outputs(lr_raw[1], lr_w, 1, slice(0, D))
         gw0 = new_weights(0)
@@ -248,8 +251,9 @@ def tile_tttinner_pb_kernel(tc, err, train_view, test_view, W, b, lr_w, lr_b, ou
             quantise(ge[:], e_codes[:, gt, half(1)], e_scales[:, gt, half(1)])
             column_sums(sums[1], 1, gt)
         quantise_weights(0, gw0)
+        scale_sums(1, sums[1])
         transpose_rates(1)
-        bias_and_residual(1, sums[1])
+        bias_and_residual(1)
         gw1 = new_weights(1)
 
         gq = [transpose_query(c) for c in range(2)]

@@ -23,7 +23,7 @@ def tile_tttinner_pb_kernel(tc, err, train_view, test_view, W, b, lr_w, lr_b, ou
     nc = tc.nc
     with ExitStack() as ctx:
         const = ctx.enter_context(tc.tile_pool(name="const", bufs=1))
-        rawp = ctx.enter_context(tc.tile_pool(name="rawp", bufs=6))
+        rawp = ctx.enter_context(tc.tile_pool(name="rawp", bufs=8))
         grp = ctx.enter_context(tc.tile_pool(name="grp", bufs=6))
         gqp = ctx.enter_context(tc.tile_pool(name="gqp", bufs=2))
         tmpp = ctx.enter_context(tc.tile_pool(name="tmpp", bufs=4))
@@ -85,11 +85,11 @@ def tile_tttinner_pb_kernel(tc, err, train_view, test_view, W, b, lr_w, lr_b, ou
         def quantise(grouped, codes, scales):
             V.quantize_mx(out=codes.bitcast(FP8X4), scales=scales, in_=grouped)
 
-        def regroup_train(gt, g, eng):
+        def regroup_train(gt, g, engs):
             gr = grouped_tile()
             for u in range(2):
                 c0 = H * g + Q * u
-                copy_on(eng, gr[:, 4 * Q * u:4 * Q * (u + 1)].rearrange("p (e q j) -> p q e j", e=2, j=4),
+                copy_on(engs[u], gr[:, 4 * Q * u:4 * Q * (u + 1)].rearrange("p (e q j) -> p q e j", e=2, j=4),
                         trn_raw[gt][:, :, c0:c0 + Q].rearrange("p j (q e) -> p q e j", e=2))
             return gr
 
@@ -144,6 +144,14 @@ def tile_tttinner_pb_kernel(tc, err, train_view, test_view, W, b, lr_w, lr_b, ou
                                      lhsT_scale=t_scales[:, gt, w0:w0 + P],
                                      rhs=e_codes[:, gt, oc].bitcast(FP8X4), rhs_scale=e_scales[:, gt, oc],
                                      start=(gt == 0), stop=(gt == 1))
+            tmp = tmpp.tile([P, 2, H], F32, tag="tmp", name="tmp")
+            for u in range(2):
+                V.scalar_tensor_tensor(out=tmp[:, u, :].rearrange("p (o e) -> p o e", e=2),
+                                       in0=accs[u][:].rearrange("p (e o) -> p o e", e=2), scalar=-C,
+                                       in1=lrT_bf[:, 2 * g + u, oc, :], op0=ALU.mult, op1=ALU.mult)
+            return tmp
+
+        def weights(g, oq):
             wp = ps.tile([P, H], F32, tag="bank", name="tp_w")
             for u in range(2):
                 for k in range(2):
@@ -151,12 +159,7 @@ def tile_tttinner_pb_kernel(tc, err, train_view, test_view, W, b, lr_w, lr_b, ou
                     PE.transpose(wp[:, Q * u + P * k:Q * u + P * k + P],
                                  w_raw[oq // 2][:, 2 * (oq % 2) + k, :].bitcast(F32)[:, P * wb:P * wb + P],
                                  ident[:])
-            tmp = tmpp.tile([P, 2, H], F32, tag="tmp", name="tmp")
-            for u in range(2):
-                V.scalar_tensor_tensor(out=tmp[:, u, :].rearrange("p (o e) -> p o e", e=2),
-                                       in0=accs[u][:].rearrange("p (e o) -> p o e", e=2), scalar=-C,
-                                       in1=lrT_bf[:, 2 * g + u, oc, :], op0=ALU.mult, op1=ALU.mult)
-            return tmp, wp
+            return wp
 
         def add(gw, oq, tmp, wp):
             c0 = 4 * Q * (oq % 2)
@@ -170,11 +173,11 @@ def tile_tttinner_pb_kernel(tc, err, train_view, test_view, W, b, lr_w, lr_b, ou
             waiting = None
             for g in range(2):
                 for oq in (2 * h, 2 * h + 1):
-                    product = multiply(g, oq)
+                    tmp = multiply(g, oq)
                     if waiting is not None:
-                        add(*waiting)
-                    waiting = (grouped[g], oq) + product
-            add(*waiting)
+                        add(grouped[waiting[0]], waiting[1], waiting[2], weights(waiting[0], waiting[1]))
+                    waiting = (g, oq, tmp)
+            add(grouped[waiting[0]], waiting[1], waiting[2], weights(waiting[0], waiting[1]))
             return grouped
 
         def quantise_weights(h, grouped):
@@ -222,28 +225,29 @@ def tile_tttinner_pb_kernel(tc, err, train_view, test_view, W, b, lr_w, lr_b, ou
 
         sums = [ps.tile([P, H], F32, tag="bank", name="sums0")]
         for gt in range(2):
-            gr0 = regroup_train(gt, 0, V)
-            gr1 = regroup_train(gt, 1, S)
-            ge = regroup_err(gt, 0, ((V, 0, Q), (S, Q, H)))
+            gr0 = regroup_train(gt, 0, (V, V))
+            gr1 = regroup_train(gt, 1, (V, S) if gt == 0 else (S, S))
+            cut = Q if gt == 0 else H - P
+            ge = regroup_err(gt, 0, ((V, 0, cut), (S, cut, H)))
             quantise(gr0[:], t_codes[:, gt, half(0)], t_scales[:, gt, half(0)])
-            quantise(gr1[:], t_codes[:, gt, half(1)], t_scales[:, gt, half(1)])
             quantise(ge[:], e_codes[:, gt, half(0)], e_scales[:, gt, half(0)])
+            quantise(gr1[:], t_codes[:, gt, half(1)], t_scales[:, gt, half(1)])
             column_sums(sums[0], 0, gt)
         for gt in range(2):
             load_tokens(err_raw[gt], err, gt, half(1))
-        q_raw = []
-        for c in range(2):
-            q_raw.append(raw_tile("q_raw%d" % c))
-            nc.sync.dma_start(out=q_raw[c][:], in_=q_view[:, 4 * c:4 * c + 4, :])
+        q_raw = [raw_tile("q_raw0")]
+        nc.sync.dma_start(out=q_raw[0][:], in_=q_view[:, 0:4, :])
+        lr_raw.append(raw_tile("lr_raw1"))
+        load_outputs(lr_raw[1], lr_w, 1, slice(0, D))
+        q_raw.append(raw_tile("q_raw1"))
+        nc.sync.dma_start(out=q_raw[1][:], in_=q_view[:, 4:8, :])
+        w_raw.append(raw_tile("w_raw1"))
+        load_outputs(w_raw[1], W, 1, slice(0, D))
 
         scale_sums(0, sums[0])
         transpose_rates(0)
         bias_and_residual(0)
-        lr_raw.append(raw_tile("lr_raw1"))
-        load_outputs(lr_raw[1], lr_w, 1, slice(0, D))
         gw0 = new_weights(0)
-        w_raw.append(raw_tile("w_raw1"))
-        load_outputs(w_raw[1], W, 1, slice(0, D))
 
         sums.append(ps.tile([P, H], F32, tag="bank", name="sums1"))
         for gt in range(2):

@@ -23,7 +23,8 @@ def tile_tttinner_pb_kernel(tc, err, train_view, test_view, W, b, lr_w, lr_b, ou
     nc = tc.nc
     with ExitStack() as ctx:
         const = ctx.enter_context(tc.tile_pool(name="const", bufs=1))
-        rawp = ctx.enter_context(tc.tile_pool(name="rawp", bufs=8))
+        rawp = ctx.enter_context(tc.tile_pool(name="rawp", bufs=6))
+        errp = ctx.enter_context(tc.tile_pool(name="errp", bufs=4))
         grp = ctx.enter_context(tc.tile_pool(name="grp", bufs=6))
         gqp = ctx.enter_context(tc.tile_pool(name="gqp", bufs=2))
         tmpp = ctx.enter_context(tc.tile_pool(name="tmpp", bufs=4))
@@ -67,11 +68,25 @@ def tile_tttinner_pb_kernel(tc, err, train_view, test_view, W, b, lr_w, lr_b, ou
         def raw_tile(nm):
             return rawp.tile([P, 4, D], BF16, tag="raw", name=nm)
 
-        def load_tokens(dst, x, gt, cols):
-            nc.sync.dma_start(out=dst[:, :, cols], in_=x[half(gt), cols].rearrange("(p j) w -> p j w", j=4))
+        def load_train(gt):
+            raw = raw_tile("trn_raw")
+            nc.sync.dma_start(out=raw[:], in_=train_view[half(gt), :].rearrange("(p j) w -> p j w", j=4))
+            return raw
 
-        def load_outputs(dst, x, h, cols):
-            nc.sync.dma_start(out=dst[:, :, cols], in_=x[half(h), cols].rearrange("(a p) d -> p a d", p=P))
+        def load_err(gt, h):
+            raw = errp.tile([P, 4, H], BF16, tag="err", name="err_raw")
+            nc.sync.dma_start(out=raw[:], in_=err[half(gt), half(h)].rearrange("(p j) w -> p j w", j=4))
+            return raw
+
+        def load_outputs(x, h):
+            raw = raw_tile("out_raw")
+            nc.sync.dma_start(out=raw[:], in_=x[half(h), :].rearrange("(p a) d -> p a d", a=4))
+            return raw
+
+        def load_query(c):
+            raw = raw_tile("q_raw")
+            nc.sync.dma_start(out=raw[:], in_=q_view[:, 4 * c:4 * c + 4, :])
+            return raw
 
         def copy_on(eng, dst, src):
             if eng is V:
@@ -85,38 +100,38 @@ def tile_tttinner_pb_kernel(tc, err, train_view, test_view, W, b, lr_w, lr_b, ou
         def quantise(grouped, codes, scales):
             V.quantize_mx(out=codes.bitcast(FP8X4), scales=scales, in_=grouped)
 
-        def regroup_train(gt, g, engs):
-            gr = grouped_tile()
-            for u in range(2):
-                c0 = H * g + Q * u
-                copy_on(engs[u], gr[:, 4 * Q * u:4 * Q * (u + 1)].rearrange("p (e q j) -> p q e j", e=2, j=4),
-                        trn_raw[gt][:, :, c0:c0 + Q].rearrange("p j (q e) -> p q e j", e=2))
-            return gr
+        def regroup_train(gr, gt, g, u, eng):
+            c0 = H * g + Q * u
+            copy_on(eng, gr[:, 4 * Q * u:4 * Q * (u + 1)].rearrange("p (e q j) -> p q e j", e=2, j=4),
+                    trn_raw[gt][:, :, c0:c0 + Q].rearrange("p j (q e) -> p q e j", e=2))
 
-        def regroup_err(gt, h, shares):
-            ge = grouped_tile()
-            for eng, c0, c1 in shares:
-                copy_on(eng, ge[:, 4 * c0:4 * c1].rearrange("p (c i t) -> p c t i", i=4, t=4),
-                        err_raw[gt][:, :, H * h + c0:H * h + c1].rearrange("p t (c i) -> p c t i", i=4))
-            return ge
+        def regroup_err(ge, gt, h, i0, i1, eng):
+            copy_on(eng, ge[:, H * i0:H * i1].rearrange("p (i c t) -> p c t i", c=P, t=4),
+                    err_raw[gt, h][:].rearrange("p t (c i) -> p c t i", i=4)[:, :, :, i0:i1])
 
-        def column_sums(acc, h, gt):
+        def quantise_train(gr, gt, g):
+            quantise(gr[:], t_codes[:, gt, half(g)], t_scales[:, gt, half(g)])
+
+        def quantise_err(ge, gt, h):
+            quantise(ge[:], e_codes[:, gt, half(h)], e_scales[:, gt, half(h)])
+
+        def column_sums(h, gt):
             for j in range(4):
-                PE.matmul(out=acc[:], lhsT=ones[:], rhs=err_raw[gt][:, j, half(h)],
+                PE.matmul(out=sums[h][:], lhsT=ones[:], rhs=err_raw[gt, h][:, j, :],
                           start=(gt == 0 and j == 0), stop=(gt == 1 and j == 3))
 
-        def transpose_rates(h):
-            for wb in range(4):
+        def transpose_rates(h, words):
+            for wb in words:
                 tp = ps.tile([P, H], F32, tag="bank", name="tp_lr")
                 for ab in range(4):
                     PE.transpose(tp[:, P * ab:P * ab + P],
                                  lr_raw[h][:, ab, :].bitcast(F32)[:, P * wb:P * wb + P], ident[:])
                 S.copy(out=lrT[:, D * wb + H * h:D * wb + H * h + H], in_=tp[:])
 
-        def scale_sums(h, sums):
-            S.mul(out=gbs[:, half(h)], in_=sums[:], mul=-C)
+        def scale_sums(h):
+            S.mul(out=gbs[:, half(h)], in_=sums[h][:], mul=-C)
 
-        def bias_and_residual(h):
+        def spread_rows(h):
             spread = []
             for k in (h, 2 + h):
                 pb = ps.tile([P, H], F32, tag="bank", name="pb")
@@ -124,18 +139,26 @@ def tile_tttinner_pb_kernel(tc, err, train_view, test_view, W, b, lr_w, lr_b, ou
                 PE.matmul(out=pb[:], lhsT=ones[:], rhs=zr[:, H * k:H * k + H], start=True, stop=True)
             S.copy(out=b_bc[:, half(h)], in_=spread[0][:])
             S.copy(out=lrb[:, half(h)], in_=spread[1][:])
+
+        def new_bias(h):
             G.tensor_tensor(out=gbs[:, half(h)], in0=gbs[:, half(h)], in1=lrb[:, half(h)], op=ALU.mult)
             G.tensor_tensor(out=b_bc[:, half(h)], in0=gbs[:, half(h)], in1=b_bc[:, half(h)], op=ALU.add)
-            for a in range(8):
+
+        def residual(h, tokens):
+            for a in tokens:
                 G.tensor_tensor(out=qb[:, a, half(h)], in0=q_raw[a // 4][:, a % 4, half(h)], in1=b_bc[:, half(h)],
                                 op=ALU.add)
 
-        def multiply(g, oq):
+        def unit(k):
+            return (k // 2) % 2, 2 * (k // 4) + k % 2
+
+        def pe_products(k):
+            g, oq = unit(k)
             oc = slice(Q * oq, Q * oq + Q)
-            accs = []
+            accs[k] = []
             for u in range(2):
                 acc = ps.tile([P, H], F32, tag="bank", name="acc1")
-                accs.append(acc)
+                accs[k].append(acc)
                 for e in range(2):
                     w0 = H * g + Q * u + P * e
                     for gt in range(2):
@@ -144,126 +167,188 @@ def tile_tttinner_pb_kernel(tc, err, train_view, test_view, W, b, lr_w, lr_b, ou
                                      lhsT_scale=t_scales[:, gt, w0:w0 + P],
                                      rhs=e_codes[:, gt, oc].bitcast(FP8X4), rhs_scale=e_scales[:, gt, oc],
                                      start=(gt == 0), stop=(gt == 1))
-            tmp = tmpp.tile([P, 2, H], F32, tag="tmp", name="tmp")
-            for u in range(2):
-                V.scalar_tensor_tensor(out=tmp[:, u, :].rearrange("p (o e) -> p o e", e=2),
-                                       in0=accs[u][:].rearrange("p (e o) -> p o e", e=2), scalar=-C,
-                                       in1=lrT_bf[:, 2 * g + u, oc, :], op0=ALU.mult, op1=ALU.mult)
-            return tmp
 
-        def weights(g, oq):
+        def v_multiply(k):
+            g, oq = unit(k)
+            oc = slice(Q * oq, Q * oq + Q)
+            tmps[k] = tmpp.tile([P, 2, H], F32, tag="tmp", name="tmp")
+            for u in range(2):
+                V.scalar_tensor_tensor(out=tmps[k][:, u, :].rearrange("p (o e) -> p o e", e=2),
+                                       in0=accs[k][u][:].rearrange("p (e o) -> p o e", e=2), scalar=-C,
+                                       in1=lrT_bf[:, 2 * g + u, oc, :], op0=ALU.mult, op1=ALU.mult)
+
+        def pe_weights(k):
+            g, oq = unit(k)
             wp = ps.tile([P, H], F32, tag="bank", name="tp_w")
+            wps[k] = wp
             for u in range(2):
                 for k in range(2):
                     wb = 2 * g + u
                     PE.transpose(wp[:, Q * u + P * k:Q * u + P * k + P],
                                  w_raw[oq // 2][:, 2 * (oq % 2) + k, :].bitcast(F32)[:, P * wb:P * wb + P],
                                  ident[:])
-            return wp
 
-        def add(gw, oq, tmp, wp):
+        def v_add(k):
+            g, oq = unit(k)
+            h = k // 4
+            if (h, g) not in gw:
+                gw[h, g] = grouped_tile()
             c0 = 4 * Q * (oq % 2)
-            V.tensor_tensor(out=gw[:, c0:c0 + 4 * Q].rearrange("p (o u e) -> p o u e", u=2, e=2),
-                            in0=tmp[:].rearrange("p u (o e) -> p o u e", e=2),
-                            in1=wp[:].bitcast(BF16).rearrange("p (u o e) -> p o u e", u=2, e=2),
+            V.tensor_tensor(out=gw[h, g][:, c0:c0 + 4 * Q].rearrange("p (o u e) -> p o u e", u=2, e=2),
+                            in0=tmps[k][:].rearrange("p u (o e) -> p o u e", e=2),
+                            in1=wps[k][:].bitcast(BF16).rearrange("p (u o e) -> p o u e", u=2, e=2),
                             op=ALU.add)
 
-        def new_weights(h):
-            grouped = [grouped_tile(), grouped_tile()]
-            waiting = None
-            for g in range(2):
-                for oq in (2 * h, 2 * h + 1):
-                    tmp = multiply(g, oq)
-                    if waiting is not None:
-                        add(grouped[waiting[0]], waiting[1], waiting[2], weights(waiting[0], waiting[1]))
-                    waiting = (g, oq, tmp)
-            add(grouped[waiting[0]], waiting[1], waiting[2], weights(waiting[0], waiting[1]))
-            return grouped
+        def quantise_weights(h, g):
+            quantise(gw[h, g][:], w_codes[:, g, half(h)], w_scales[:, g, half(h)])
 
-        def quantise_weights(h, grouped):
-            for g in range(2):
-                quantise(grouped[g][:], w_codes[:, g, half(h)], w_scales[:, g, half(h)])
-
-        def transpose_query(c):
-            gq = gqp.tile([P, 2 * 4 * H], BF16, tag="gq", name="gq", align_bytes=64)
-            gq_w = gq[:].bitcast(F32).rearrange("p (g t u) -> p g t u", g=2, u=2)
-            for a4 in range(4):
+        def transpose_query(c, blocks):
+            if c not in gq:
+                gq[c] = gqp.tile([P, 2 * 4 * H], BF16, tag="gq", name="gq", align_bytes=64)
+            gq_w = gq[c][:].bitcast(F32).rearrange("p (g t u) -> p g t u", g=2, u=2)
+            for a4 in blocks:
                 tp = ps.tile([P, 4, P], F32, tag="bank", name="tp_q")
                 for wb in range(4):
                     PE.transpose(tp[:, wb, :], q_raw[c][:, a4, :].bitcast(F32)[:, P * wb:P * wb + P], ident[:])
                 S.copy(out=gq_w[:, :, P * a4:P * a4 + P, :], in_=tp[:].rearrange("p (g u) t -> p g t u", g=2))
-            return gq
 
-        def query(h):
-            for a in range(8):
-                acc = ps.tile([P, H], F32, tag="bank", name="acc2")
-                for g in range(2):
-                    PE.matmul_mx(out=acc[:],
-                                 lhsT=q_codes[:, g, P * a:P * a + P].bitcast(FP8X4),
-                                 lhsT_scale=q_scales[:, g, P * a:P * a + P],
-                                 rhs=w_codes[:, g, half(h)].bitcast(FP8X4), rhs_scale=w_scales[:, g, half(h)],
-                                 start=(g == 0), stop=(g == 1))
-                V.tensor_tensor(out=qb[:, a, half(h)], in0=acc[:], in1=qb[:, a, half(h)], op=ALU.add)
-                if h == 1 and a >= 6:
-                    nc.sync.dma_start(out=out_v[:, a, half(h)], in_=qb[:, a, half(h)])
-                elif a % 2 == 1:
-                    nc.sync.dma_start(out=out_v[:, a - 1:a + 1, half(h)], in_=qb[:, a - 1:a + 1, half(h)])
-
-        trn_raw = [raw_tile("trn_raw0"), raw_tile("trn_raw1")]
-        err_raw = [raw_tile("err_raw0"), raw_tile("err_raw1")]
-        lr_raw = [raw_tile("lr_raw0")]
-        w_raw = [raw_tile("w_raw0")]
-        load_tokens(trn_raw[0], train_view, 0, slice(0, D))
-        load_tokens(err_raw[0], err, 0, half(0))
-        nc.sync.dma_start(out=zr[0:1, 0:D], in_=b.rearrange("(o d) -> o d", o=1))
-        nc.sync.dma_start(out=zr[0:1, D:2 * D], in_=lr_b.rearrange("(o d) -> o d", o=1))
-        load_tokens(trn_raw[1], train_view, 1, slice(0, D))
-        load_tokens(err_raw[1], err, 1, half(0))
-        load_outputs(lr_raw[0], lr_w, 0, half(0))
-        load_outputs(lr_raw[0], lr_w, 0, half(1))
-        load_outputs(w_raw[0], W, 0, slice(0, D))
-
-        sums = [ps.tile([P, H], F32, tag="bank", name="sums0")]
-        for gt in range(2):
-            gr0 = regroup_train(gt, 0, (V, V))
-            gr1 = regroup_train(gt, 1, (V, S) if gt == 0 else (S, S))
-            cut = Q if gt == 0 else H - P
-            ge = regroup_err(gt, 0, ((V, 0, cut), (S, cut, H)))
-            quantise(gr0[:], t_codes[:, gt, half(0)], t_scales[:, gt, half(0)])
-            quantise(ge[:], e_codes[:, gt, half(0)], e_scales[:, gt, half(0)])
-            quantise(gr1[:], t_codes[:, gt, half(1)], t_scales[:, gt, half(1)])
-            column_sums(sums[0], 0, gt)
-        for gt in range(2):
-            load_tokens(err_raw[gt], err, gt, half(1))
-        q_raw = [raw_tile("q_raw0")]
-        nc.sync.dma_start(out=q_raw[0][:], in_=q_view[:, 0:4, :])
-        lr_raw.append(raw_tile("lr_raw1"))
-        load_outputs(lr_raw[1], lr_w, 1, slice(0, D))
-        q_raw.append(raw_tile("q_raw1"))
-        nc.sync.dma_start(out=q_raw[1][:], in_=q_view[:, 4:8, :])
-        w_raw.append(raw_tile("w_raw1"))
-        load_outputs(w_raw[1], W, 1, slice(0, D))
-
-        scale_sums(0, sums[0])
-        transpose_rates(0)
-        bias_and_residual(0)
-        gw0 = new_weights(0)
-
-        sums.append(ps.tile([P, H], F32, tag="bank", name="sums1"))
-        for gt in range(2):
-            ge = regroup_err(gt, 1, ((S, 0, H),))
-            quantise(ge[:], e_codes[:, gt, half(1)], e_scales[:, gt, half(1)])
-            column_sums(sums[1], 1, gt)
-        quantise_weights(0, gw0)
-        scale_sums(1, sums[1])
-        transpose_rates(1)
-        bias_and_residual(1)
-        gw1 = new_weights(1)
-
-        gq = [transpose_query(c) for c in range(2)]
-        quantise_weights(1, gw1)
-        for c in range(2):
+        def quantise_query(c):
             for g in range(2):
                 quantise(gq[c][:, 4 * H * g:4 * H * (g + 1)], q_codes[:, g, half(c)], q_scales[:, g, half(c)])
-        for h in range(2):
-            query(h)
+
+        def query(h, a):
+            acc = ps.tile([P, H], F32, tag="bank", name="acc2")
+            answers[h, a] = acc
+            for g in range(2):
+                PE.matmul_mx(out=acc[:],
+                             lhsT=q_codes[:, g, P * a:P * a + P].bitcast(FP8X4),
+                             lhsT_scale=q_scales[:, g, P * a:P * a + P],
+                             rhs=w_codes[:, g, half(h)].bitcast(FP8X4), rhs_scale=w_scales[:, g, half(h)],
+                             start=(g == 0), stop=(g == 1))
+
+        def finish(h, a):
+            row = qb[:, a, half(h)].rearrange("p (c i) -> p c i", i=4)
+            V.tensor_tensor(out=row, in0=answers[h, a][:].rearrange("p (i c) -> p c i", i=4), in1=row, op=ALU.add)
+
+        def store(a, n, cols):
+            nc.sync.dma_start(out=out_v[:, a:a + n, cols], in_=qb[:, a:a + n, cols])
+
+        accs = {}
+        tmps = {}
+        wps = {}
+        gw = {}
+        gq = {}
+        answers = {}
+        trn_raw = {}
+        err_raw = {}
+        lr_raw = {}
+        w_raw = {}
+        q_raw = {}
+        trn_raw[0] = load_train(0)
+        err_raw[0, 0] = load_err(0, 0)
+        trn_raw[1] = load_train(1)
+        err_raw[1, 0] = load_err(1, 0)
+        nc.sync.dma_start(out=zr[0:1, 0:D], in_=b.rearrange("(o d) -> o d", o=1))
+        nc.sync.dma_start(out=zr[0:1, D:2 * D], in_=lr_b.rearrange("(o d) -> o d", o=1))
+        lr_raw[0] = load_outputs(lr_w, 0)
+        w_raw[0] = load_outputs(W, 0)
+        q_raw[0] = load_query(0)
+        err_raw[0, 1] = load_err(0, 1)
+        err_raw[1, 1] = load_err(1, 1)
+        lr_raw[1] = load_outputs(lr_w, 1)
+        q_raw[1] = load_query(1)
+        w_raw[1] = load_outputs(W, 1)
+
+        sums = [ps.tile([P, H], F32, tag="bank", name="sums0")]
+        gr0 = grouped_tile()
+        gr1 = grouped_tile()
+        ge = grouped_tile()
+        regroup_train(gr0, 0, 0, 0, V)
+        regroup_train(gr0, 0, 0, 1, V)
+        regroup_train(gr1, 0, 1, 0, V)
+        regroup_train(gr1, 0, 1, 1, S)
+        regroup_err(ge, 0, 0, 0, 2, V)
+        regroup_err(ge, 0, 0, 2, 4, S)
+        quantise_train(gr0, 0, 0)
+        quantise_train(gr1, 0, 1)
+        quantise_err(ge, 0, 0)
+        column_sums(0, 0)
+        gr0 = grouped_tile()
+        gr1 = grouped_tile()
+        ge = grouped_tile()
+        regroup_train(gr0, 1, 0, 0, V)
+        regroup_train(gr0, 1, 0, 1, V)
+        regroup_train(gr1, 1, 1, 0, S)
+        regroup_train(gr1, 1, 1, 1, S)
+        regroup_err(ge, 1, 0, 0, 3, V)
+        regroup_err(ge, 1, 0, 3, 4, S)
+        quantise_train(gr0, 1, 0)
+        quantise_err(ge, 1, 0)
+        quantise_train(gr1, 1, 1)
+        column_sums(0, 1)
+        scale_sums(0)
+        spread_rows(0)
+        transpose_rates(0, range(2))
+        new_bias(0)
+        pe_products(0)
+        v_multiply(0)
+        pe_products(1)
+        pe_weights(0)
+        v_multiply(1)
+        v_add(0)
+        transpose_rates(0, range(2, 4))
+        residual(0, range(8))
+        pe_products(2)
+        pe_weights(1)
+        v_multiply(2)
+        v_add(1)
+        pe_products(3)
+        pe_weights(2)
+        v_multiply(3)
+        v_add(2)
+        sums.append(ps.tile([P, H], F32, tag="bank", name="sums1"))
+        for gt in range(2):
+            ge = grouped_tile()
+            regroup_err(ge, gt, 1, 0, 4, S)
+            quantise_err(ge, gt, 1)
+        pe_weights(3)
+        v_add(3)
+        for gt in range(2):
+            column_sums(1, gt)
+        quantise_weights(0, 0)
+        quantise_weights(0, 1)
+        scale_sums(1)
+        transpose_rates(1, range(4))
+        spread_rows(1)
+        new_bias(1)
+        residual(1, range(8))
+        pe_products(4)
+        v_multiply(4)
+        pe_products(5)
+        pe_weights(4)
+        v_multiply(5)
+        v_add(4)
+        pe_products(6)
+        pe_weights(5)
+        v_multiply(6)
+        v_add(5)
+        pe_products(7)
+        pe_weights(6)
+        v_multiply(7)
+        v_add(6)
+        pe_weights(7)
+        transpose_query(0, range(4))
+        transpose_query(1, range(4))
+        v_add(7)
+        quantise_weights(1, 0)
+        quantise_weights(1, 1)
+        quantise_query(0)
+        quantise_query(1)
+        for a in range(8):
+            for h in range(2):
+                query(h, a)
+                finish(h, a)
+                if a == 7:
+                    store(a, 1, half(h))
+            if a < 7:
+                store(a, 1, slice(0, D))

@@ -102,8 +102,8 @@ def tile_tttinner_pb_kernel(tc, err, train_view, test_view, W, b, lr_w, lr_b, ou
 
         def regroup_train(gr, gt, g, u, eng):
             c0 = H * g + Q * u
-            copy_on(eng, gr[:, 4 * Q * u:4 * Q * (u + 1)].rearrange("p (e q j) -> p q e j", e=2, j=4),
-                    trn_raw[gt][:, :, c0:c0 + Q].rearrange("p j (q e) -> p q e j", e=2))
+            copy_on(eng, gr[:, 4 * Q * u:4 * Q * (u + 1)].rearrange("p (e k q j) -> p k j q e", e=2, q=2, j=4),
+                    trn_raw[gt][:, :, c0:c0 + Q].rearrange("p j (k q e) -> p k j q e", q=2, e=2))
 
         def regroup_err(ge, gt, h, i0, i1, eng):
             copy_on(eng, ge[:, H * i0:H * i1].rearrange("p (i c t) -> p c t i", c=P, t=4),

@@ -43,6 +43,8 @@ def tile_tttinner_pb_kernel(tc, err, train_view, test_view, W, b, lr_w, lr_b, ou
         V.memset(zr[:], 0.0)
         ones = const.tile([P, P], BF16)
         V.memset(ones[:], 1.0)
+        minus_c = const.tile([P, P], BF16)
+        V.memset(minus_c[:], -C)
         ident = const.tile([P, P], F32)
         make_identity(nc, ident[:])
         warm = const.tile([P, 1], F32)
@@ -117,7 +119,7 @@ def tile_tttinner_pb_kernel(tc, err, train_view, test_view, W, b, lr_w, lr_b, ou
 
         def column_sums(h, gt):
             for j in range(4):
-                PE.matmul(out=sums[h][:], lhsT=ones[:], rhs=err_raw[gt, h][:, j, :],
+                PE.matmul(out=sums[h][:], lhsT=minus_c[:], rhs=err_raw[gt, h][:, j, :],
                           start=(gt == 0 and j == 0), stop=(gt == 1 and j == 3))
 
         def transpose_rates(h, words):
@@ -129,7 +131,7 @@ def tile_tttinner_pb_kernel(tc, err, train_view, test_view, W, b, lr_w, lr_b, ou
                 S.copy(out=lrT[:, D * wb + H * h:D * wb + H * h + H], in_=tp[:])
 
         def scale_sums(h):
-            S.mul(out=gbs[:, half(h)], in_=sums[h][:], mul=-C)
+            S.copy(out=gbs[:, half(h)], in_=sums[h][:])
 
         def spread_rows(h):
             spread = []

@@ -309,12 +309,14 @@ def tile_tttinner_pb_kernel(tc, err, train_view, test_view, W, b, lr_w, lr_b, ou
         v_multiply(3)
         v_add(2)
         sums.append(ps.tile([P, H], F32, tag="bank", name="sums1"))
-        for gt in range(2):
-            ge = grouped_tile()
-            regroup_err(ge, gt, 1, 0, 4, S)
-            quantise_err(ge, gt, 1)
+        ge0 = grouped_tile()
+        ge1 = grouped_tile()
+        regroup_err(ge0, 0, 1, 0, 4, S)
+        regroup_err(ge1, 1, 1, 0, 4, S)
         pe_weights(3)
         v_add(3)
+        quantise_err(ge0, 0, 1)
+        quantise_err(ge1, 1, 1)
         for gt in range(2):
             column_sums(1, gt)
         quantise_weights(0, 0)
@@ -332,25 +334,26 @@ def tile_tttinner_pb_kernel(tc, err, train_view, test_view, W, b, lr_w, lr_b, ou
         v_add(4)
         pe_products(6)
         pe_weights(5)
+        transpose_query(0, range(2))
         v_multiply(6)
         v_add(5)
         pe_products(7)
         pe_weights(6)
+        transpose_query(0, range(2, 4))
         v_multiply(7)
         v_add(6)
         pe_weights(7)
-        transpose_query(0, range(4))
         transpose_query(1, range(4))
         v_add(7)
+        quantise_query(0)
         quantise_weights(1, 0)
         quantise_weights(1, 1)
-        quantise_query(0)
         quantise_query(1)
         for a in range(8):
             for h in range(2):
                 query(h, a)
                 finish(h, a)
-                if a == 7:
+                if a in (0, 7):
                     store(a, 1, half(h))
-            if a < 7:
+            if 0 < a < 7:
                 store(a, 1, slice(0, D))

from contextlib import ExitStack

import concourse.mybir as mybir
from concourse.masks import make_identity

F32 = mybir.dt.float32
BF16 = mybir.dt.bfloat16
U32 = mybir.dt.uint32
U8 = mybir.dt.uint8
FP8X4 = mybir.dt.float8_e4m3fn_x4
ALU = mybir.AluOpType

P = 128
T = 1024
D = 1024
H = 512
Q = 256
C = 2.0 / (T * D)
FLOPS = 4 * T * D * D


def tile_tttinner_pb_kernel(tc, err, train_view, test_view, W, b, lr_w, lr_b, out):
    nc = tc.nc
    with ExitStack() as ctx:
        const = ctx.enter_context(tc.tile_pool(name="const", bufs=1))
        rawp = ctx.enter_context(tc.tile_pool(name="rawp", bufs=6))
        errp = ctx.enter_context(tc.tile_pool(name="errp", bufs=4))
        grp = ctx.enter_context(tc.tile_pool(name="grp", bufs=6))
        gqp = ctx.enter_context(tc.tile_pool(name="gqp", bufs=2))
        tmpp = ctx.enter_context(tc.tile_pool(name="tmpp", bufs=4))
        ps = ctx.enter_context(tc.psum_pool(name="ps", bufs=8))
        ctx.enter_context(tc.manual_schedule())

        V = nc.vector
        S = nc.scalar
        G = nc.gpsimd
        PE = nc.tensor

        def half(h):
            return slice(H * h, H * h + H)

        zr = const.tile([P, 2 * D], BF16)
        V.memset(zr[:], 0.0)
        ones = const.tile([P, P], BF16)
        V.memset(ones[:], 1.0)
        minus_c = const.tile([P, P], BF16)
        V.memset(minus_c[:], -C)
        ident = const.tile([P, P], F32)
        make_identity(nc, ident[:])
        warm = const.tile([P, 1], F32)
        G.tensor_tensor(out=warm[:], in0=ident[:, 0:1], in1=ident[:, 0:1], op=ALU.add)

        e_codes = const.tile([P, 2, D], U32, align_bytes=64)
        e_scales = const.tile([P, 2, D], U8, align_bytes=64)
        t_codes = const.tile([P, 2, D], U32, align_bytes=64)
        t_scales = const.tile([P, 2, D], U8, align_bytes=64)
        w_codes = const.tile([P, 2, D], U32, align_bytes=64)
        w_scales = const.tile([P, 2, D], U8, align_bytes=64)
        q_codes = const.tile([P, 2, T], U32, align_bytes=64)
        q_scales = const.tile([P, 2, T], U8, align_bytes=64)
        lrT = const.tile([P, 4 * D], F32)
        lrT_bf = lrT[:].bitcast(BF16).rearrange("p (w o e) -> p w o e", w=4, e=2)
        qb = const.tile([P, 8, D], F32)
        b_bc = const.tile([P, D], F32)
        lrb = const.tile([P, D], F32)
        gbs = const.tile([P, D], F32)
        q_view = test_view.rearrange("(p a) d -> p a d", a=8)
        out_v = out.rearrange("(p a) d -> p a d", a=8)

        def raw_tile(nm):
            return rawp.tile([P, 4, D], BF16, tag="raw", name=nm)

        def load_train(gt):
            raw = raw_tile("trn_raw")
            nc.sync.dma_start(out=raw[:], in_=train_view[half(gt), :].rearrange("(p j) w -> p j w", j=4))
            return raw

        def load_err(gt, h):
            raw = errp.tile([P, 4, H], BF16, tag="err", name="err_raw")
            nc.sync.dma_start(out=raw[:], in_=err[half(gt), half(h)].rearrange("(p j) w -> p j w", j=4))
            return raw

        def load_outputs(x, h):
            raw = raw_tile("out_raw")
            nc.sync.dma_start(out=raw[:], in_=x[half(h), :].rearrange("(p a) d -> p a d", a=4))
            return raw

        def load_query(c):
            raw = raw_tile("q_raw")
            nc.sync.dma_start(out=raw[:], in_=q_view[:, 4 * c:4 * c + 4, :])
            return raw

        def copy_on(eng, dst, src):
            if eng is V:
                V.tensor_copy(out=dst, in_=src)
            else:
                S.copy(out=dst, in_=src)

        def grouped_tile():
            return grp.tile([P, 4 * H], BF16, tag="grp", name="grouped", align_bytes=64)

        def quantise(grouped, codes, scales):
            V.quantize_mx(out=codes.bitcast(FP8X4), scales=scales, in_=grouped)

        def regroup_train(gr, gt, g, u, eng):
            c0 = H * g + Q * u
            copy_on(eng, gr[:, 4 * Q * u:4 * Q * (u + 1)].rearrange("p (e k q j) -> p k j q e", e=2, q=2, j=4),
                    trn_raw[gt][:, :, c0:c0 + Q].rearrange("p j (k q e) -> p k j q e", q=2, e=2))

        def regroup_err(ge, gt, h, i0, i1, eng):
            copy_on(eng, ge[:, H * i0:H * i1].rearrange("p (i c t) -> p c t i", c=P, t=4),
                    err_raw[gt, h][:].rearrange("p t (c i) -> p c t i", i=4)[:, :, :, i0:i1])

        def quantise_train(gr, gt, g):
            quantise(gr[:], t_codes[:, gt, half(g)], t_scales[:, gt, half(g)])

        def quantise_err(ge, gt, h):
            quantise(ge[:], e_codes[:, gt, half(h)], e_scales[:, gt, half(h)])

        def column_sums(h, gt):
            for j in range(4):
                PE.matmul(out=sums[h][:], lhsT=minus_c[:], rhs=err_raw[gt, h][:, j, :],
                          start=(gt == 0 and j == 0), stop=(gt == 1 and j == 3))

        def transpose_rates(h, words):
            for wb in words:
                tp = ps.tile([P, H], F32, tag="bank", name="tp_lr")
                for ab in range(4):
                    PE.transpose(tp[:, P * ab:P * ab + P],
                                 lr_raw[h][:, ab, :].bitcast(F32)[:, P * wb:P * wb + P], ident[:])
                S.copy(out=lrT[:, D * wb + H * h:D * wb + H * h + H], in_=tp[:])

        def scale_sums(h):
            S.copy(out=gbs[:, half(h)], in_=sums[h][:])

        def spread_rows(h):
            spread = []
            for k in (h, 2 + h):
                pb = ps.tile([P, H], F32, tag="bank", name="pb")
                spread.append(pb)
                PE.matmul(out=pb[:], lhsT=ones[:], rhs=zr[:, H * k:H * k + H], start=True, stop=True)
            S.copy(out=b_bc[:, half(h)], in_=spread[0][:])
            S.copy(out=lrb[:, half(h)], in_=spread[1][:])

        def new_bias(h):
            G.tensor_tensor(out=gbs[:, half(h)], in0=gbs[:, half(h)], in1=lrb[:, half(h)], op=ALU.mult)
            G.tensor_tensor(out=b_bc[:, half(h)], in0=gbs[:, half(h)], in1=b_bc[:, half(h)], op=ALU.add)

        def residual(h, tokens):
            for a in tokens:
                G.tensor_tensor(out=qb[:, a, half(h)], in0=q_raw[a // 4][:, a % 4, half(h)], in1=b_bc[:, half(h)],
                                op=ALU.add)

        def unit(k):
            return (k // 2) % 2, 2 * (k // 4) + k % 2

        def pe_products(k):
            g, oq = unit(k)
            oc = slice(Q * oq, Q * oq + Q)
            accs[k] = []
            for u in range(2):
                acc = ps.tile([P, H], F32, tag="bank", name="acc1")
                accs[k].append(acc)
                for e in range(2):
                    w0 = H * g + Q * u + P * e
                    for gt in range(2):
                        PE.matmul_mx(out=acc[:, Q * e:Q * e + Q],
                                     lhsT=t_codes[:, gt, w0:w0 + P].bitcast(FP8X4),
                                     lhsT_scale=t_scales[:, gt, w0:w0 + P],
                                     rhs=e_codes[:, gt, oc].bitcast(FP8X4), rhs_scale=e_scales[:, gt, oc],
                                     start=(gt == 0), stop=(gt == 1))

        def v_multiply(k):
            g, oq = unit(k)
            oc = slice(Q * oq, Q * oq + Q)
            tmps[k] = tmpp.tile([P, 2, H], F32, tag="tmp", name="tmp")
            for u in range(2):
                V.scalar_tensor_tensor(out=tmps[k][:, u, :].rearrange("p (o e) -> p o e", e=2),
                                       in0=accs[k][u][:].rearrange("p (e o) -> p o e", e=2), scalar=-C,
                                       in1=lrT_bf[:, 2 * g + u, oc, :], op0=ALU.mult, op1=ALU.mult)

        def pe_weights(k):
            g, oq = unit(k)
            wp = ps.tile([P, H], F32, tag="bank", name="tp_w")
            wps[k] = wp
            for u in range(2):
                for k in range(2):
                    wb = 2 * g + u
                    PE.transpose(wp[:, Q * u + P * k:Q * u + P * k + P],
                                 w_raw[oq // 2][:, 2 * (oq % 2) + k, :].bitcast(F32)[:, P * wb:P * wb + P],
                                 ident[:])

        def v_add(k):
            g, oq = unit(k)
            h = k // 4
            if (h, g) not in gw:
                gw[h, g] = grouped_tile()
            c0 = 4 * Q * (oq % 2)
            V.tensor_tensor(out=gw[h, g][:, c0:c0 + 4 * Q].rearrange("p (o u e) -> p o u e", u=2, e=2),
                            in0=tmps[k][:].rearrange("p u (o e) -> p o u e", e=2),
                            in1=wps[k][:].bitcast(BF16).rearrange("p (u o e) -> p o u e", u=2, e=2),
                            op=ALU.add)

        def quantise_weights(h, g):
            quantise(gw[h, g][:], w_codes[:, g, half(h)], w_scales[:, g, half(h)])

        def transpose_query(c, blocks):
            if c not in gq:
                gq[c] = gqp.tile([P, 2 * 4 * H], BF16, tag="gq", name="gq", align_bytes=64)
            gq_w = gq[c][:].bitcast(F32).rearrange("p (g t u) -> p g t u", g=2, u=2)
            for a4 in blocks:
                tp = ps.tile([P, 4, P], F32, tag="bank", name="tp_q")
                for wb in range(4):
                    PE.transpose(tp[:, wb, :], q_raw[c][:, a4, :].bitcast(F32)[:, P * wb:P * wb + P], ident[:])
                S.copy(out=gq_w[:, :, P * a4:P * a4 + P, :], in_=tp[:].rearrange("p (g u) t -> p g t u", g=2))

        def quantise_query(c):
            for g in range(2):
                quantise(gq[c][:, 4 * H * g:4 * H * (g + 1)], q_codes[:, g, half(c)], q_scales[:, g, half(c)])

        def query(h, a):
            acc = ps.tile([P, H], F32, tag="bank", name="acc2")
            answers[h, a] = acc
            for g in range(2):
                PE.matmul_mx(out=acc[:],
                             lhsT=q_codes[:, g, P * a:P * a + P].bitcast(FP8X4),
                             lhsT_scale=q_scales[:, g, P * a:P * a + P],
                             rhs=w_codes[:, g, half(h)].bitcast(FP8X4), rhs_scale=w_scales[:, g, half(h)],
                             start=(g == 0), stop=(g == 1))

        def finish(h, a):
            row = qb[:, a, half(h)].rearrange("p (c i) -> p c i", i=4)
            V.tensor_tensor(out=row, in0=answers[h, a][:].rearrange("p (i c) -> p c i", i=4), in1=row, op=ALU.add)

        def store(a, n, cols):
            nc.sync.dma_start(out=out_v[:, a:a + n, cols], in_=qb[:, a:a + n, cols])

        accs = {}
        tmps = {}
        wps = {}
        gw = {}
        gq = {}
        answers = {}
        trn_raw = {}
        err_raw = {}
        lr_raw = {}
        w_raw = {}
        q_raw = {}
        trn_raw[0] = load_train(0)
        err_raw[0, 0] = load_err(0, 0)
        trn_raw[1] = load_train(1)
        err_raw[1, 0] = load_err(1, 0)
        nc.sync.dma_start(out=zr[0:1, 0:D], in_=b.rearrange("(o d) -> o d", o=1))
        nc.sync.dma_start(out=zr[0:1, D:2 * D], in_=lr_b.rearrange("(o d) -> o d", o=1))
        lr_raw[0] = load_outputs(lr_w, 0)
        w_raw[0] = load_outputs(W, 0)
        q_raw[0] = load_query(0)
        err_raw[0, 1] = load_err(0, 1)
        err_raw[1, 1] = load_err(1, 1)
        lr_raw[1] = load_outputs(lr_w, 1)
        q_raw[1] = load_query(1)
        w_raw[1] = load_outputs(W, 1)

        sums = [ps.tile([P, H], F32, tag="bank", name="sums0")]
        gr0 = grouped_tile()
        gr1 = grouped_tile()
        ge = grouped_tile()
        regroup_train(gr0, 0, 0, 0, V)
        regroup_train(gr0, 0, 0, 1, V)
        regroup_train(gr1, 0, 1, 0, V)
        regroup_train(gr1, 0, 1, 1, S)
        regroup_err(ge, 0, 0, 0, 2, V)
        regroup_err(ge, 0, 0, 2, 4, S)
        quantise_train(gr0, 0, 0)
        quantise_train(gr1, 0, 1)
        quantise_err(ge, 0, 0)
        column_sums(0, 0)
        gr0 = grouped_tile()
        gr1 = grouped_tile()
        ge = grouped_tile()
        regroup_train(gr0, 1, 0, 0, V)
        regroup_train(gr0, 1, 0, 1, V)
        regroup_train(gr1, 1, 1, 0, S)
        regroup_train(gr1, 1, 1, 1, S)
        regroup_err(ge, 1, 0, 0, 3, V)
        regroup_err(ge, 1, 0, 3, 4, S)
        quantise_train(gr0, 1, 0)
        quantise_err(ge, 1, 0)
        quantise_train(gr1, 1, 1)
        column_sums(0, 1)
        scale_sums(0)
        spread_rows(0)
        transpose_rates(0, range(2))
        new_bias(0)
        pe_products(0)
        v_multiply(0)
        pe_products(1)
        pe_weights(0)
        v_multiply(1)
        v_add(0)
        transpose_rates(0, range(2, 4))
        residual(0, range(8))
        pe_products(2)
        pe_weights(1)
        v_multiply(2)
        v_add(1)
        pe_products(3)
        pe_weights(2)
        v_multiply(3)
        v_add(2)
        sums.append(ps.tile([P, H], F32, tag="bank", name="sums1"))
        ge0 = grouped_tile()
        ge1 = grouped_tile()
        regroup_err(ge0, 0, 1, 0, 4, S)
        regroup_err(ge1, 1, 1, 0, 4, S)
        pe_weights(3)
        v_add(3)
        quantise_err(ge0, 0, 1)
        quantise_err(ge1, 1, 1)
        for gt in range(2):
            column_sums(1, gt)
        quantise_weights(0, 0)
        quantise_weights(0, 1)
        scale_sums(1)
        transpose_rates(1, range(4))
        spread_rows(1)
        new_bias(1)
        residual(1, range(8))
        pe_products(4)
        v_multiply(4)
        pe_products(5)
        pe_weights(4)
        v_multiply(5)
        v_add(4)
        pe_products(6)
        pe_weights(5)
        transpose_query(0, range(2))
        v_multiply(6)
        v_add(5)
        pe_products(7)
        pe_weights(6)
        transpose_query(0, range(2, 4))
        v_multiply(7)
        v_add(6)
        pe_weights(7)
        transpose_query(1, range(4))
        v_add(7)
        quantise_query(0)
        quantise_weights(1, 0)
        quantise_weights(1, 1)
        quantise_query(1)
        for a in range(8):
            for h in range(2):
                query(h, a)
                finish(h, a)
                if a in (0, 7):
                    store(a, 1, half(h))
            if 0 < a < 7:
                store(a, 1, slice(0, D))
